import numpy as np
import ml_dtypes


def mxq(x, axis, fmt="e4m3"):
    dtype, down = {"e4m3": (ml_dtypes.float8_e4m3fn, 7), "e5m2": (ml_dtypes.float8_e5m2, 14)}[fmt]
    v = np.moveaxis(np.asarray(x, np.float32).astype(ml_dtypes.bfloat16).astype(np.float64), axis, -1)
    blocks = v.reshape(v.shape[:-1] + (-1, 32))
    amax = np.abs(blocks).max(-1, keepdims=True)
    byte = np.maximum(np.where(amax > 0, np.frexp(amax)[1] - 1 + 127, 0) - down, 1)
    scale = np.exp2(byte - 127.0)
    codes = (blocks / scale).astype(np.float32).astype(dtype).astype(np.float64)
    return np.moveaxis((codes * scale).reshape(v.shape), -1, axis)


WIDE = False


def mx_kscale(k):
    if not WIDE:
        return np.ones(k)
    levels = np.array([10, -10, 5, -5, 0])
    a = np.random.permutation(np.resize(levels, k // 512 * 4)).reshape(k // 512, 4)
    idx = np.arange(k)
    return np.exp2(a[idx // 512, idx % 128 // 32])


BF16 = ml_dtypes.bfloat16


def bf(x):
    return np.asarray(x, np.float32).astype(BF16)


def f64(x):
    return np.asarray(x).astype(np.float64)


B, E, P, H, HK, D = 16, 256, 768, 4, 2, 128
G = H // HK
S = P + E
SCALING = 1.0 / np.sqrt(D)


def setup_inputs():
    s = mx_kscale(S)
    a = np.log2(s)
    g = s.max() / s
    q = np.random.standard_normal((B, E, H, D)) * 2.0
    k = np.random.standard_normal((B, E, HK, D))
    v = np.random.standard_normal((B, E, HK, D)) * 2.0
    k_cache = np.random.standard_normal((B, P, HK, D))
    v_cache = np.random.standard_normal((B, P, HK, D)) * 2.0
    q[..., 0] = np.log(2.0) * np.sqrt(D)
    k_cache[..., 0] += a[:P][None, :, None]
    k[..., 0] += a[P:][None, :, None]
    v_cache *= g[:P][None, :, None, None]
    v *= g[P:][None, :, None, None]
    return {"q": bf(q), "k": bf(k), "v": bf(v), "k_cache": bf(k_cache), "v_cache": bf(v_cache)}


def reference(q, k, v, k_cache, v_cache):
    k_all = np.concatenate([f64(k_cache), f64(k)], axis=1)
    v_all = np.concatenate([f64(v_cache), f64(v)], axis=1)
    qg = f64(q).reshape(B, E, HK, G, D).transpose(0, 2, 3, 1, 4).reshape(B, HK, G * E, D)
    scores = ((qg @ k_all.transpose(0, 2, 3, 1)) * SCALING).reshape(B, HK, G, E, S)
    visible = np.arange(S)[None, :] <= (P + np.arange(E))[:, None]
    scores = np.where(visible[None, None, None, :, :], scores, -1e30)
    e = np.exp(scores - scores.max(-1, keepdims=True))
    o = mxq(e, 4, "e4m3").reshape(B, HK, G * E, S) @ mxq(v_all, 1, "e4m3").transpose(0, 2, 1, 3)
    o = o.reshape(B, HK, G, E, D) / e.sum(-1, keepdims=True)
    return o.transpose(0, 3, 1, 2, 4).reshape(B * E, H * D)

@@ -1,0 +1,355 @@
+from contextlib import ExitStack
+import math
+
+import concourse.bass as bass
+import concourse.mybir as mybir
+import concourse.tile as tile
+from concourse.masks import make_identity
+
+FP8X4 = mybir.dt.float8_e4m3fn_x4
+BF16 = mybir.dt.bfloat16
+F32 = mybir.dt.float32
+U32 = mybir.dt.uint32
+U8 = mybir.dt.uint8
+ALU = mybir.AluOpType
+ACTF = mybir.ActivationFunctionType
+AX = mybir.AxisListType
+
+B, E, PRE, H, HK, D = 16, 256, 768, 4, 2, 128
+S = PRE + E
+P = 128
+SCALING = 1.0 / math.sqrt(D)
+NEG = -1.0e30
+FLOPS = 2 * 2 * B * H * E * S * D
+
+NU = B * 8
+VIA_GPSIMD = (0, 1, 2, 3, 4, 5, 6)
+C_ON_VECTOR = ()
+PREP_ON_VECTOR = (True, True, True)
+MANUAL = False
+
+
+def tile_radixattention_t_kernel(tc, q, k, v, k_cache, v_cache, out):
+    nc = tc.nc
+    with ExitStack() as ctx:
+        if MANUAL:
+            ctx.enter_context(tc.manual_schedule())
+        const = ctx.enter_context(tc.tile_pool(name="const", bufs=1))
+        raw = ctx.enter_context(tc.tile_pool(name="raw", bufs=4))
+        prep = ctx.enter_context(tc.tile_pool(name="prep", bufs=2))
+        work = ctx.enter_context(tc.tile_pool(name="work", bufs=4))
+        small = ctx.enter_context(tc.tile_pool(name="small", bufs=6))
+        ps_s = ctx.enter_context(tc.psum_pool(name="ps_s", bufs=4))
+        ps_t = ctx.enter_context(tc.psum_pool(name="ps_t", bufs=2))
+        ps_o = ctx.enter_context(tc.psum_pool(name="ps_o", bufs=2))
+
+        q_v = q.rearrange("b (qb p) h d -> b p qb (h d)", p=P)
+        k_v = k.rearrange("b (c p) hk d -> b p c (hk d)", p=P)
+        kc_v = k_cache.rearrange("b (c p) hk d -> b p c (hk d)", p=P)
+        v_v = v.rearrange("b (c p) hk d -> b p c (hk d)", p=P)
+        vc_v = v_cache.rearrange("b (c p) hk d -> b p c (hk d)", p=P)
+
+        kraw_t, qraw_t, vraw_t = {}, {}, {}
+        kt_t, qt_t, vg_t, vcod_t, vsc_t = {}, {}, {}, {}, {}
+
+        def load(b):
+            kraw = raw.tile([P, 8, HK * D], BF16, tag="kraw")
+            nc.sync.dma_start(out=kraw[:, 0:6, :], in_=kc_v[b])
+            nc.sync.dma_start(out=kraw[:, 6:8, :], in_=k_v[b])
+            qraw = raw.tile([P, 2, H * D], BF16, tag="qraw")
+            nc.sync.dma_start(out=qraw[:], in_=q_v[b])
+            vraw = raw.tile([P, 8, HK * D], BF16, tag="vraw")
+            nc.sync.dma_start(out=vraw[:, 0:6, :], in_=vc_v[b])
+            nc.sync.dma_start(out=vraw[:, 6:8, :], in_=v_v[b])
+            kraw_t[b], qraw_t[b], vraw_t[b] = kraw, qraw, vraw
+
+        for b in range(3):
+            load(b)
+
+        ident = const.tile([P, P], BF16, name="ident")
+        make_identity(nc, ident[:])
+        mask32 = const.tile([P, P], F32, name="mask32")
+        nc.gpsimd.memset(mask32[:], 0.0)
+        nc.gpsimd.affine_select(
+            out=mask32[:],
+            in_=mask32[:],
+            compare_op=ALU.is_ge,
+            fill=NEG,
+            base=0,
+            pattern=[[-1, P]],
+            channel_multiplier=1,
+        )
+        mask = const.tile([P, P], BF16, name="mask")
+        nc.vector.tensor_copy(out=mask[:], in_=mask32[:])
+        plz = []
+        for i in range(3):
+            plzi = const.tile([P, S], BF16, name="plz%d" % i)
+            nc.vector.memset(plzi[:, S - P : S], 0.0)
+            plz.append(plzi)
+        warm = const.tile([P, 1], F32, name="warm")
+        nc.vector.memset(warm[:], 0.0)
+        warm2 = const.tile([P, 1], F32, name="warm2")
+        nc.scalar.activation(out=warm2[:], in_=warm[:], func=ACTF.Exp)
+
+        def copy_out(on_vector, dst, src):
+            if on_vector:
+                nc.vector.tensor_copy(out=dst, in_=src)
+            else:
+                nc.scalar.copy(out=dst, in_=src)
+
+        def prep_k(b, hk, on_vector):
+            if hk == 0:
+                kt = prep.tile([P, HK, S], BF16, tag="kt")
+                kt_t[b] = kt
+            tp = ps_t.tile([P, S], BF16, tag="t")
+            for c in range(8):
+                nc.tensor.transpose(
+                    out=tp[:, c * P : (c + 1) * P],
+                    in_=kraw_t[b][:, c, hk * D : (hk + 1) * D],
+                    identity=ident[:],
+                )
+            copy_out(on_vector, kt_t[b][:, hk, :], tp[:])
+
+        def prep_q(b, on_vector):
+            qt = prep.tile([P, 8, P], BF16, tag="qt")
+            qt_t[b] = qt
+            tp = ps_t.tile([P, S], BF16, tag="t")
+            for i in range(8):
+                nc.tensor.transpose(
+                    out=tp[:, i * P : (i + 1) * P],
+                    in_=qraw_t[b][:, i // 4, (i % 4) * D : (i % 4 + 1) * D],
+                    identity=ident[:],
+                )
+            copy_out(on_vector, qt[:].rearrange("p i c -> p (i c)"), tp[:])
+
+        def prep_v_group(b):
+            vg = prep.tile([P, 2, HK * D, 4], BF16, tag="vg", align_bytes=64)
+            vg_t[b] = vg
+            nc.gpsimd.tensor_scalar(
+                out=vg[:],
+                in0=vraw_t[b][:].rearrange("p (g t) x -> p g x t", g=2),
+                scalar1=1.0,
+                scalar2=0.0,
+                op0=ALU.mult,
+                op1=ALU.add,
+            )
+
+        def prep_v_quant(b):
+            vcod = prep.tile([P, 2 * HK * D], U32, tag="vcod", align_bytes=64)
+            vsc = prep.tile([P, 2 * HK * D], U8, tag="vsc", align_bytes=64)
+            vcod_t[b], vsc_t[b] = vcod, vsc
+            nc.vector.quantize_mx(
+                out=vcod[:].bitcast(FP8X4),
+                scales=vsc[:],
+                in_=vg_t[b][:].rearrange("p g x t -> p (g x t)"),
+            )
+
+        st = {}
+
+        def unit(u):
+            return u // 8, (u % 8) // 4, u % 4
+
+        def stage_s(u):
+            b, qb, h = unit(u)
+            hk = h // 2
+            qt = qt_t[b][:, qb * 4 + h, :]
+            kt = kt_t[b]
+            s_a = ps_s.tile([P, 512], F32, tag="s")
+            s_b = ps_s.tile([P, 512], F32, tag="s")
+            nc.tensor.matmul(out=s_a[:], lhsT=qt, rhs=kt[:, hk, 0:512], start=True, stop=True)
+            nfree = 256 + qb * P
+            nc.tensor.matmul(
+                out=s_b[:, 0:nfree], lhsT=qt, rhs=kt[:, hk, 512 : 512 + nfree], start=True, stop=True
+            )
+            nc.tensor.matmul(
+                out=s_b[:, nfree : nfree + P],
+                lhsT=qt,
+                rhs=kt[:, hk, 512 + nfree : 512 + nfree + P],
+                start=True,
+                stop=False,
+            )
+            nc.tensor.matmul(
+                out=s_b[:, nfree : nfree + P], lhsT=ident[:], rhs=mask[:], start=False, stop=True
+            )
+            st[u] = {"s_a": s_a, "s_b": s_b, "nb": nfree + P}
+
+        def stage_m(u):
+            d = st[u]
+            mx = small.tile([P, 2], F32, tag="mx")
+            nc.vector.tensor_reduce(out=mx[:, 0:1], in_=d["s_a"][:], axis=AX.X, op=ALU.max)
+            nc.vector.tensor_reduce(
+                out=mx[:, 1:2], in_=d["s_b"][:, 0 : d["nb"]], axis=AX.X, op=ALU.max
+            )
+            bias = small.tile([P, 1], F32, tag="bias")
+            nc.vector.tensor_scalar(
+                out=bias[:],
+                in0=mx[:, 0:1],
+                scalar1=mx[:, 1:2],
+                scalar2=-SCALING,
+                op0=ALU.max,
+                op1=ALU.mult,
+            )
+            d["bias"] = bias
+
+        sums = {}
+
+        def stage_e(u):
+            b, qb, h = unit(u)
+            d = st[u]
+            if h == 0:
+                ssum = small.tile([P, 4, 2], F32, tag="ssum")
+                sums[u // 4] = ssum
+            ssum = sums[u // 4]
+            e = work.tile([P, S], BF16, tag="e")
+            nc.scalar.activation(
+                out=e[:, 0:512],
+                in_=d["s_a"][:],
+                func=ACTF.Exp,
+                bias=d["bias"][:],
+                scale=SCALING,
+                accum_out=ssum[:, h, 0:1],
+            )
+            nc.scalar.activation(
+                out=e[:, 512 : 512 + d["nb"]],
+                in_=d["s_b"][:, 0 : d["nb"]],
+                func=ACTF.Exp,
+                bias=d["bias"][:],
+                scale=SCALING,
+                accum_out=ssum[:, h, 1:2],
+            )
+            d["e"] = e
+
+        def stage_t(u):
+            d = st[u]
+            tp = ps_t.tile([P, S], BF16, tag="t")
+            for j in range(4 + d["nb"] // P):
+                nc.tensor.transpose(
+                    out=tp[:, j * P : (j + 1) * P],
+                    in_=d["e"][:, j * P : (j + 1) * P],
+                    identity=ident[:],
+                )
+            d["tp"] = tp
+
+        def stage_c(u):
+            b, qb, h = unit(u)
+            d = st[u]
+            if (u % 8) in VIA_GPSIMD:
+                if qb == 0:
+                    pl = plz[(b * 4 + h) % 3]
+                else:
+                    pl = work.tile([P, S], BF16, tag="pl")
+                n = 512 + d["nb"]
+                copy_out((u % 8) in C_ON_VECTOR, pl[:, 0:n], d["tp"][:, 0:n])
+                d["pl"] = pl
+            else:
+                gq = work.tile([P, 2, P, 4], BF16, tag="gq", align_bytes=64)
+                copy_out(
+                    (u % 8) in C_ON_VECTOR,
+                    gq[:],
+                    d["tp"][:].rearrange("p (g t c) -> p g c t", g=2, t=4),
+                )
+                d["gq"] = gq
+
+        def stage_g(u):
+            d = st[u]
+            if (u % 8) in VIA_GPSIMD:
+                gq = work.tile([P, 2, P, 4], BF16, tag="gq", align_bytes=64)
+                nc.gpsimd.tensor_scalar(
+                    out=gq[:],
+                    in0=d["pl"][:].rearrange("p (g t c) -> p g c t", g=2, t=4),
+                    scalar1=1.0,
+                    scalar2=0.0,
+                    op0=ALU.mult,
+                    op1=ALU.add,
+                )
+                d["gq"] = gq
+
+        def stage_q(u):
+            d = st[u]
+            ecod = work.tile([P, 2 * P], U32, tag="ecod", align_bytes=64)
+            esc = work.tile([P, 2 * P], U8, tag="esc", align_bytes=64)
+            nc.vector.quantize_mx(
+                out=ecod[:].bitcast(FP8X4),
+                scales=esc[:],
+                in_=d["gq"][:].rearrange("p g c t -> p (g c t)"),
+            )
+            d["ecod"], d["esc"] = ecod, esc
+
+        outs = {}
+
+        def stage_x(u):
+            b, qb, h = unit(u)
+            hk = h // 2
+            d = st[u]
+            if h == 0:
+                o_ps = ps_o.tile([P, H * D], F32, tag="o")
+                outs[u // 4] = o_ps
+            o_ps = outs[u // 4]
+            for g in range(2):
+                vcols = slice((g * HK + hk) * D, (g * HK + hk + 1) * D)
+                nc.tensor.matmul_mx(
+                    out=o_ps[:, h * D : (h + 1) * D],
+                    lhsT=d["ecod"][:, g * P : (g + 1) * P].bitcast(FP8X4),
+                    lhsT_scale=d["esc"][:, g * P : (g + 1) * P],
+                    rhs=vcod_t[b][:, vcols].bitcast(FP8X4),
+                    rhs_scale=vsc_t[b][:, vcols],
+                    start=(g == 0),
+                    stop=(g == 1),
+                )
+
+        def stage_n(su):
+            b, qb = su // 2, su % 2
+            rs = small.tile([P, 4], F32, tag="rs")
+            nc.vector.tensor_reduce(out=rs[:], in_=sums[su][:], axis=AX.X, op=ALU.add)
+            rinv = small.tile([P, 4], F32, tag="rinv")
+            nc.vector.reciprocal(out=rinv[:], in_=rs[:])
+            o_sb = work.tile([P, H, D], F32, tag="o_sb")
+            nc.vector.tensor_tensor(
+                out=o_sb[:],
+                in0=outs[su][:].rearrange("p (h d) -> p h d", h=H),
+                in1=rinv[:].unsqueeze(2).to_broadcast([P, H, D]),
+                op=ALU.mult,
+            )
+            r0 = b * E + qb * P
+            nc.sync.dma_start(out=out[r0 : r0 + P, :], in_=o_sb[:].rearrange("p h d -> p (h d)"))
+
+        prep_k(0, 0, True)
+        prep_q(0, False)
+        prep_k(0, 1, True)
+        prep_v_group(0)
+        prep_v_quant(0)
+
+        for step in range(-1, NU + 6):
+            if 0 <= step - 5 < NU:
+                stage_x(step - 5)
+            if 0 <= step - 2 < NU:
+                stage_t(step - 2)
+            if 0 <= step - 1 < NU:
+                stage_e(step - 1)
+            nb_ = step // 8 + 1
+            if 0 <= step < NU and nb_ < B:
+                i = step % 8
+                if i == 0:
+                    prep_k(nb_, 0, PREP_ON_VECTOR[0])
+                    if nb_ + 2 < B:
+                        load(nb_ + 2)
+                elif i == 1:
+                    prep_v_group(nb_)
+                elif i == 2:
+                    prep_k(nb_, 1, PREP_ON_VECTOR[1])
+                elif i == 4:
+                    prep_q(nb_, PREP_ON_VECTOR[2])
+                elif i == 5:
+                    prep_v_quant(nb_)
+            if 0 <= step + 1 < NU:
+                stage_s(step + 1)
+            if 0 <= step < NU:
+                stage_m(step)
+            if 0 <= step - 2 < NU:
+                stage_c(step - 2)
+            if 0 <= step - 3 < NU:
+                stage_g(step - 3)
+            if 0 <= step - 4 < NU:
+                stage_q(step - 4)
+            if 0 <= step - 5 < NU and (step - 5) % 4 == 3:
+                stage_n((step - 5) // 4)

@@ -23,10 +23,9 @@ NEG = -1.0e30
 FLOPS = 2 * 2 * B * H * E * S * D
 
 NU = B * 8
-VIA_GPSIMD = (0, 1, 2, 3, 4, 5, 6)
-C_ON_VECTOR = ()
-PREP_ON_VECTOR = (True, True, True)
-MANUAL = False
+C_ON_VECTOR = (0, 3, 6)
+PREP_ON_VECTOR = (False, False, False)
+MANUAL = True
 
 
 def tile_radixattention_t_kernel(tc, q, k, v, k_cache, v_cache, out):
@@ -40,8 +39,8 @@ def tile_radixattention_t_kernel(tc, q, k, v, k_cache, v_cache, out):
         work = ctx.enter_context(tc.tile_pool(name="work", bufs=4))
         small = ctx.enter_context(tc.tile_pool(name="small", bufs=6))
         ps_s = ctx.enter_context(tc.psum_pool(name="ps_s", bufs=4))
-        ps_t = ctx.enter_context(tc.psum_pool(name="ps_t", bufs=2))
-        ps_o = ctx.enter_context(tc.psum_pool(name="ps_o", bufs=2))
+        ps_t = ctx.enter_context(tc.psum_pool(name="ps_t", bufs=3))
+        ps_o = ctx.enter_context(tc.psum_pool(name="ps_o", bufs=1))
 
         q_v = q.rearrange("b (qb p) h d -> b p qb (h d)", p=P)
         k_v = k.rearrange("b (c p) hk d -> b p c (hk d)", p=P)
@@ -81,11 +80,11 @@ def tile_radixattention_t_kernel(tc, q, k, v, k_cache, v_cache, out):
         )
         mask = const.tile([P, P], BF16, name="mask")
         nc.vector.tensor_copy(out=mask[:], in_=mask32[:])
-        plz = []
+        ez = []
         for i in range(3):
-            plzi = const.tile([P, S], BF16, name="plz%d" % i)
-            nc.vector.memset(plzi[:, S - P : S], 0.0)
-            plz.append(plzi)
+            ezi = const.tile([P, S], BF16, name="ez%d" % i)
+            nc.vector.memset(ezi[:, S - P : S], 0.0)
+            ez.append(ezi)
         warm = const.tile([P, 1], F32, name="warm")
         nc.vector.memset(warm[:], 0.0)
         warm2 = const.tile([P, 1], F32, name="warm2")
@@ -108,7 +107,7 @@ def tile_radixattention_t_kernel(tc, q, k, v, k_cache, v_cache, out):
                     in_=kraw_t[b][:, c, hk * D : (hk + 1) * D],
                     identity=ident[:],
                 )
-            copy_out(on_vector, kt_t[b][:, hk, :], tp[:])
+            return lambda: copy_out(on_vector, kt_t[b][:, hk, :], tp[:])
 
         def prep_q(b, on_vector):
             qt = prep.tile([P, 8, P], BF16, tag="qt")
@@ -120,7 +119,7 @@ def tile_radixattention_t_kernel(tc, q, k, v, k_cache, v_cache, out):
                     in_=qraw_t[b][:, i // 4, (i % 4) * D : (i % 4 + 1) * D],
                     identity=ident[:],
                 )
-            copy_out(on_vector, qt[:].rearrange("p i c -> p (i c)"), tp[:])
+            return lambda: copy_out(on_vector, qt[:].rearrange("p i c -> p (i c)"), tp[:])
 
         def prep_v_group(b):
             vg = prep.tile([P, 2, HK * D, 4], BF16, tag="vg", align_bytes=64)
@@ -149,14 +148,21 @@ def tile_radixattention_t_kernel(tc, q, k, v, k_cache, v_cache, out):
         def unit(u):
             return u // 8, (u % 8) // 4, u % 4
 
-        def stage_s(u):
+        def stage_s_a(u):
             b, qb, h = unit(u)
             hk = h // 2
             qt = qt_t[b][:, qb * 4 + h, :]
             kt = kt_t[b]
             s_a = ps_s.tile([P, 512], F32, tag="s")
-            s_b = ps_s.tile([P, 512], F32, tag="s")
             nc.tensor.matmul(out=s_a[:], lhsT=qt, rhs=kt[:, hk, 0:512], start=True, stop=True)
+            st[u] = {"s_a": s_a}
+
+        def stage_s_b(u):
+            b, qb, h = unit(u)
+            hk = h // 2
+            qt = qt_t[b][:, qb * 4 + h, :]
+            kt = kt_t[b]
+            s_b = ps_s.tile([P, 512], F32, tag="s")
             nfree = 256 + qb * P
             nc.tensor.matmul(
                 out=s_b[:, 0:nfree], lhsT=qt, rhs=kt[:, hk, 512 : 512 + nfree], start=True, stop=True
@@ -171,7 +177,8 @@ def tile_radixattention_t_kernel(tc, q, k, v, k_cache, v_cache, out):
             nc.tensor.matmul(
                 out=s_b[:, nfree : nfree + P], lhsT=ident[:], rhs=mask[:], start=False, stop=True
             )
-            st[u] = {"s_a": s_a, "s_b": s_b, "nb": nfree + P}
+            st[u]["s_b"] = s_b
+            st[u]["nb"] = nfree + P
 
         def stage_m(u):
             d = st[u]
@@ -200,7 +207,10 @@ def tile_radixattention_t_kernel(tc, q, k, v, k_cache, v_cache, out):
                 ssum = small.tile([P, 4, 2], F32, tag="ssum")
                 sums[u // 4] = ssum
             ssum = sums[u // 4]
-            e = work.tile([P, S], BF16, tag="e")
+            if qb == 0:
+                e = ez[(b * 4 + h) % 3]
+            else:
+                e = work.tile([P, S], BF16, tag="e")
             nc.scalar.activation(
                 out=e[:, 0:512],
                 in_=d["s_a"][:],
@@ -222,7 +232,7 @@ def tile_radixattention_t_kernel(tc, q, k, v, k_cache, v_cache, out):
         def stage_t(u):
             d = st[u]
             tp = ps_t.tile([P, S], BF16, tag="t")
-            for j in range(4 + d["nb"] // P):
+            for j in range(8):
                 nc.tensor.transpose(
                     out=tp[:, j * P : (j + 1) * P],
                     in_=d["e"][:, j * P : (j + 1) * P],
@@ -231,38 +241,14 @@ def tile_radixattention_t_kernel(tc, q, k, v, k_cache, v_cache, out):
             d["tp"] = tp
 
         def stage_c(u):
-            b, qb, h = unit(u)
             d = st[u]
-            if (u % 8) in VIA_GPSIMD:
-                if qb == 0:
-                    pl = plz[(b * 4 + h) % 3]
-                else:
-                    pl = work.tile([P, S], BF16, tag="pl")
-                n = 512 + d["nb"]
-                copy_out((u % 8) in C_ON_VECTOR, pl[:, 0:n], d["tp"][:, 0:n])
-                d["pl"] = pl
-            else:
-                gq = work.tile([P, 2, P, 4], BF16, tag="gq", align_bytes=64)
-                copy_out(
-                    (u % 8) in C_ON_VECTOR,
-                    gq[:],
-                    d["tp"][:].rearrange("p (g t c) -> p g c t", g=2, t=4),
-                )
-                d["gq"] = gq
-
-        def stage_g(u):
-            d = st[u]
-            if (u % 8) in VIA_GPSIMD:
-                gq = work.tile([P, 2, P, 4], BF16, tag="gq", align_bytes=64)
-                nc.gpsimd.tensor_scalar(
-                    out=gq[:],
-                    in0=d["pl"][:].rearrange("p (g t c) -> p g c t", g=2, t=4),
-                    scalar1=1.0,
-                    scalar2=0.0,
-                    op0=ALU.mult,
-                    op1=ALU.add,
-                )
-                d["gq"] = gq
+            gq = work.tile([P, 2, P, 4], BF16, tag="gq", align_bytes=64)
+            copy_out(
+                (u % 8) in C_ON_VECTOR,
+                gq[:],
+                d["tp"][:].rearrange("p (g t c) -> p g c t", g=2, t=4),
+            )
+            d["gq"] = gq
 
         def stage_q(u):
             d = st[u]
@@ -313,43 +299,46 @@ def tile_radixattention_t_kernel(tc, q, k, v, k_cache, v_cache, out):
             r0 = b * E + qb * P
             nc.sync.dma_start(out=out[r0 : r0 + P, :], in_=o_sb[:].rearrange("p h d -> p (h d)"))
 
-        prep_k(0, 0, True)
-        prep_q(0, False)
-        prep_k(0, 1, True)
+        prep_k(0, 0, True)()
+        prep_q(0, False)()
+        prep_k(0, 1, True)()
         prep_v_group(0)
         prep_v_quant(0)
 
-        for step in range(-1, NU + 6):
-            if 0 <= step - 5 < NU:
-                stage_x(step - 5)
-            if 0 <= step - 2 < NU:
-                stage_t(step - 2)
+        for step in range(-1, NU + 5):
+            nxt = step // 8 + 1
+            i = step % 8
+            prepare = 0 <= step < NU and nxt < B
+            late = None
             if 0 <= step - 1 < NU:
                 stage_e(step - 1)
-            nb_ = step // 8 + 1
-            if 0 <= step < NU and nb_ < B:
-                i = step % 8
-                if i == 0:
-                    prep_k(nb_, 0, PREP_ON_VECTOR[0])
-                    if nb_ + 2 < B:
-                        load(nb_ + 2)
-                elif i == 1:
-                    prep_v_group(nb_)
-                elif i == 2:
-                    prep_k(nb_, 1, PREP_ON_VECTOR[1])
-                elif i == 4:
-                    prep_q(nb_, PREP_ON_VECTOR[2])
-                elif i == 5:
-                    prep_v_quant(nb_)
+            if 0 <= step - 2 < NU:
+                stage_t(step - 2)
+            if prepare and i == 0:
+                late = prep_k(nxt, 0, PREP_ON_VECTOR[0])
+            if prepare and i == 2:
+                late = prep_q(nxt, PREP_ON_VECTOR[1])
+            if prepare and i == 4:
+                late = prep_k(nxt, 1, PREP_ON_VECTOR[2])
             if 0 <= step + 1 < NU:
-                stage_s(step + 1)
+                stage_s_a(step + 1)
+            if 0 <= step - 4 < NU:
+                stage_x(step - 4)
+            if 0 <= step + 1 < NU:
+                stage_s_b(step + 1)
             if 0 <= step < NU:
                 stage_m(step)
             if 0 <= step - 2 < NU:
                 stage_c(step - 2)
             if 0 <= step - 3 < NU:
-                stage_g(step - 3)
-            if 0 <= step - 4 < NU:
-                stage_q(step - 4)
-            if 0 <= step - 5 < NU and (step - 5) % 4 == 3:
-                stage_n((step - 5) // 4)
+                stage_q(step - 3)
+            if 0 <= step - 4 < NU and (step - 4) % 4 == 3:
+                stage_n((step - 4) // 4)
+            if late is not None:
+                late()
+            if prepare and i == 0 and nxt + 2 < B:
+                load(nxt + 2)
+            if prepare and i == 1:
+                prep_v_group(nxt)
+            if prepare and i == 5:
+                prep_v_quant(nxt)

@@ -23,7 +23,7 @@ NEG = -1.0e30
 FLOPS = 2 * 2 * B * H * E * S * D
 
 NU = B * 8
-C_ON_VECTOR = (0, 3, 6)
+C_ON_VECTOR = (2, 6)
 PREP_ON_VECTOR = (False, False, False)
 MANUAL = True
 
@@ -39,7 +39,8 @@ def tile_radixattention_t_kernel(tc, q, k, v, k_cache, v_cache, out):
         work = ctx.enter_context(tc.tile_pool(name="work", bufs=4))
         small = ctx.enter_context(tc.tile_pool(name="small", bufs=6))
         ps_s = ctx.enter_context(tc.psum_pool(name="ps_s", bufs=4))
-        ps_t = ctx.enter_context(tc.psum_pool(name="ps_t", bufs=3))
+        ps_t = ctx.enter_context(tc.psum_pool(name="ps_t", bufs=2))
+        ps_p = ctx.enter_context(tc.psum_pool(name="ps_p", bufs=1))
         ps_o = ctx.enter_context(tc.psum_pool(name="ps_o", bufs=1))
 
         q_v = q.rearrange("b (qb p) h d -> b p qb (h d)", p=P)
@@ -100,26 +101,32 @@ def tile_radixattention_t_kernel(tc, q, k, v, k_cache, v_cache, out):
             if hk == 0:
                 kt = prep.tile([P, HK, S], BF16, tag="kt")
                 kt_t[b] = kt
-            tp = ps_t.tile([P, S], BF16, tag="t")
-            for c in range(8):
-                nc.tensor.transpose(
+            tp = ps_p.tile([P, S], BF16, tag="p")
+
+            def one(c):
+                return lambda: nc.tensor.transpose(
                     out=tp[:, c * P : (c + 1) * P],
                     in_=kraw_t[b][:, c, hk * D : (hk + 1) * D],
                     identity=ident[:],
                 )
-            return lambda: copy_out(on_vector, kt_t[b][:, hk, :], tp[:])
+
+            return [one(c) for c in range(8)], lambda: copy_out(on_vector, kt_t[b][:, hk, :], tp[:])
 
         def prep_q(b, on_vector):
             qt = prep.tile([P, 8, P], BF16, tag="qt")
             qt_t[b] = qt
-            tp = ps_t.tile([P, S], BF16, tag="t")
-            for i in range(8):
-                nc.tensor.transpose(
+            tp = ps_p.tile([P, S], BF16, tag="p")
+
+            def one(i):
+                return lambda: nc.tensor.transpose(
                     out=tp[:, i * P : (i + 1) * P],
                     in_=qraw_t[b][:, i // 4, (i % 4) * D : (i % 4 + 1) * D],
                     identity=ident[:],
                 )
-            return lambda: copy_out(on_vector, qt[:].rearrange("p i c -> p (i c)"), tp[:])
+
+            return [one(i) for i in range(8)], lambda: copy_out(
+                on_vector, qt[:].rearrange("p i c -> p (i c)"), tp[:]
+            )
 
         def prep_v_group(b):
             vg = prep.tile([P, 2, HK * D, 4], BF16, tag="vg", align_bytes=64)
@@ -167,6 +174,16 @@ def tile_radixattention_t_kernel(tc, q, k, v, k_cache, v_cache, out):
             nc.tensor.matmul(
                 out=s_b[:, 0:nfree], lhsT=qt, rhs=kt[:, hk, 512 : 512 + nfree], start=True, stop=True
             )
+            st[u]["s_b"] = s_b
+            st[u]["nb"] = nfree + P
+
+        def stage_s_d(u):
+            b, qb, h = unit(u)
+            hk = h // 2
+            qt = qt_t[b][:, qb * 4 + h, :]
+            kt = kt_t[b]
+            s_b = st[u]["s_b"]
+            nfree = st[u]["nb"] - P
             nc.tensor.matmul(
                 out=s_b[:, nfree : nfree + P],
                 lhsT=qt,
@@ -177,24 +194,33 @@ def tile_radixattention_t_kernel(tc, q, k, v, k_cache, v_cache, out):
             nc.tensor.matmul(
                 out=s_b[:, nfree : nfree + P], lhsT=ident[:], rhs=mask[:], start=False, stop=True
             )
-            st[u]["s_b"] = s_b
-            st[u]["nb"] = nfree + P
 
-        def stage_m(u):
+        def stage_m_a(u):
             d = st[u]
-            mx = small.tile([P, 2], F32, tag="mx")
-            nc.vector.tensor_reduce(out=mx[:, 0:1], in_=d["s_a"][:], axis=AX.X, op=ALU.max)
-            nc.vector.tensor_reduce(
-                out=mx[:, 1:2], in_=d["s_b"][:, 0 : d["nb"]], axis=AX.X, op=ALU.max
+            ssb = work.tile([P, S], F32, tag="ssb")
+            m0 = small.tile([P, 1], F32, tag="m0")
+            nc.vector.tensor_scalar(
+                out=ssb[:, 0:512],
+                in0=d["s_a"][:],
+                scalar1=-SCALING,
+                scalar2=None,
+                op0=ALU.mult,
+                op1=ALU.min,
+                accum_out=m0[:],
             )
+            d["ssb"], d["m0"] = ssb, m0
+
+        def stage_m_b(u):
+            d = st[u]
             bias = small.tile([P, 1], F32, tag="bias")
             nc.vector.tensor_scalar(
-                out=bias[:],
-                in0=mx[:, 0:1],
-                scalar1=mx[:, 1:2],
-                scalar2=-SCALING,
-                op0=ALU.max,
-                op1=ALU.mult,
+                out=d["ssb"][:, 512 : 512 + d["nb"]],
+                in0=d["s_b"][:, 0 : d["nb"]],
+                scalar1=-SCALING,
+                scalar2=d["m0"][:, 0:1],
+                op0=ALU.mult,
+                op1=ALU.min,
+                accum_out=bias[:],
             )
             d["bias"] = bias
 
@@ -204,41 +230,37 @@ def tile_radixattention_t_kernel(tc, q, k, v, k_cache, v_cache, out):
             b, qb, h = unit(u)
             d = st[u]
             if h == 0:
-                ssum = small.tile([P, 4, 2], F32, tag="ssum")
+                ssum = small.tile([P, 4], F32, tag="ssum")
                 sums[u // 4] = ssum
             ssum = sums[u // 4]
             if qb == 0:
                 e = ez[(b * 4 + h) % 3]
             else:
                 e = work.tile([P, S], BF16, tag="e")
+            n = 512 + d["nb"]
             nc.scalar.activation(
-                out=e[:, 0:512],
-                in_=d["s_a"][:],
+                out=e[:, 0:n],
+                in_=d["ssb"][:, 0:n],
                 func=ACTF.Exp,
                 bias=d["bias"][:],
-                scale=SCALING,
-                accum_out=ssum[:, h, 0:1],
-            )
-            nc.scalar.activation(
-                out=e[:, 512 : 512 + d["nb"]],
-                in_=d["s_b"][:, 0 : d["nb"]],
-                func=ACTF.Exp,
-                bias=d["bias"][:],
-                scale=SCALING,
-                accum_out=ssum[:, h, 1:2],
+                scale=-1.0,
+                accum_out=ssum[:, h : h + 1],
             )
             d["e"] = e
 
         def stage_t(u):
             d = st[u]
             tp = ps_t.tile([P, S], BF16, tag="t")
-            for j in range(8):
-                nc.tensor.transpose(
+            d["tp"] = tp
+
+            def one(j):
+                return lambda: nc.tensor.transpose(
                     out=tp[:, j * P : (j + 1) * P],
                     in_=d["e"][:, j * P : (j + 1) * P],
                     identity=ident[:],
                 )
-            d["tp"] = tp
+
+            return [one(j) for j in range(8)]
 
         def stage_c(u):
             d = st[u]
@@ -283,12 +305,16 @@ def tile_radixattention_t_kernel(tc, q, k, v, k_cache, v_cache, out):
                     stop=(g == 1),
                 )
 
+        rinvs = {}
+
+        def stage_r(su):
+            rinv = small.tile([P, 4], F32, tag="rinv")
+            nc.vector.reciprocal(out=rinv[:], in_=sums[su][:])
+            rinvs[su] = rinv
+
         def stage_n(su):
             b, qb = su // 2, su % 2
-            rs = small.tile([P, 4], F32, tag="rs")
-            nc.vector.tensor_reduce(out=rs[:], in_=sums[su][:], axis=AX.X, op=ALU.add)
-            rinv = small.tile([P, 4], F32, tag="rinv")
-            nc.vector.reciprocal(out=rinv[:], in_=rs[:])
+            rinv = rinvs[su]
             o_sb = work.tile([P, H, D], F32, tag="o_sb")
             nc.vector.tensor_tensor(
                 out=o_sb[:],
@@ -299,46 +325,66 @@ def tile_radixattention_t_kernel(tc, q, k, v, k_cache, v_cache, out):
             r0 = b * E + qb * P
             nc.sync.dma_start(out=out[r0 : r0 + P, :], in_=o_sb[:].rearrange("p h d -> p (h d)"))
 
-        prep_k(0, 0, True)()
-        prep_q(0, False)()
-        prep_k(0, 1, True)()
+        def run(calls):
+            for call in calls:
+                call()
+
+        for first in (prep_k(0, 0, True), prep_q(0, False), prep_k(0, 1, True)):
+            run(first[0])
+            first[1]()
         prep_v_group(0)
         prep_v_quant(0)
 
-        for step in range(-1, NU + 5):
+        waiting = []
+        for step in range(-1, NU + 6):
             nxt = step // 8 + 1
             i = step % 8
             prepare = 0 <= step < NU and nxt < B
             late = None
             if 0 <= step - 1 < NU:
                 stage_e(step - 1)
+            if 0 <= step < NU:
+                stage_m_a(step)
+            if 0 <= step - 5 < NU and (step - 5) % 4 == 3:
+                stage_n((step - 5) // 4)
+            tr = []
             if 0 <= step - 2 < NU:
-                stage_t(step - 2)
-            if prepare and i == 0:
-                late = prep_k(nxt, 0, PREP_ON_VECTOR[0])
-            if prepare and i == 2:
-                late = prep_q(nxt, PREP_ON_VECTOR[1])
-            if prepare and i == 4:
-                late = prep_k(nxt, 1, PREP_ON_VECTOR[2])
+                tr = stage_t(step - 2)
+            if prepare and i in (0, 2, 4):
+                if i == 0:
+                    group = prep_k(nxt, 0, PREP_ON_VECTOR[0])
+                elif i == 2:
+                    group = prep_q(nxt, PREP_ON_VECTOR[1])
+                else:
+                    group = prep_k(nxt, 1, PREP_ON_VECTOR[2])
+                waiting = group[0]
+            if prepare and i in (1, 3, 5):
+                late = group[1]
+            tr = tr + waiting[0:4]
+            waiting = waiting[4:]
             if 0 <= step + 1 < NU:
                 stage_s_a(step + 1)
-            if 0 <= step - 4 < NU:
-                stage_x(step - 4)
+            run(tr[0:6])
             if 0 <= step + 1 < NU:
                 stage_s_b(step + 1)
-            if 0 <= step < NU:
-                stage_m(step)
-            if 0 <= step - 2 < NU:
-                stage_c(step - 2)
+            run(tr[6:])
+            if 0 <= step + 1 < NU:
+                stage_s_d(step + 1)
+            if 0 <= step - 4 < NU:
+                stage_x(step - 4)
             if 0 <= step - 3 < NU:
                 stage_q(step - 3)
-            if 0 <= step - 4 < NU and (step - 4) % 4 == 3:
-                stage_n((step - 4) // 4)
+            if 0 <= step < NU:
+                stage_m_b(step)
+            if 0 <= step - 2 < NU:
+                stage_c(step - 2)
+            if 0 <= step - 2 < NU and (step - 2) % 4 == 3:
+                stage_r((step - 2) // 4)
             if late is not None:
                 late()
             if prepare and i == 0 and nxt + 2 < B:
                 load(nxt + 2)
             if prepare and i == 1:
                 prep_v_group(nxt)
-            if prepare and i == 5:
+            if prepare and i == 6:
                 prep_v_quant(nxt)

@@ -23,8 +23,8 @@ NEG = -1.0e30
 FLOPS = 2 * 2 * B * H * E * S * D
 
 NU = B * 8
-C_ON_VECTOR = (2, 6)
-PREP_ON_VECTOR = (False, False, False)
+C_ON_VECTOR = (6,)
+PREP_ON_VECTOR = (True, True, True)
 MANUAL = True
 
 
@@ -128,16 +128,13 @@ def tile_radixattention_t_kernel(tc, q, k, v, k_cache, v_cache, out):
                 on_vector, qt[:].rearrange("p i c -> p (i c)"), tp[:]
             )
 
-        def prep_v_group(b):
-            vg = prep.tile([P, 2, HK * D, 4], BF16, tag="vg", align_bytes=64)
-            vg_t[b] = vg
-            nc.gpsimd.tensor_scalar(
-                out=vg[:],
-                in0=vraw_t[b][:].rearrange("p (g t) x -> p g x t", g=2),
-                scalar1=1.0,
-                scalar2=0.0,
-                op0=ALU.mult,
-                op1=ALU.add,
+        def prep_v_group(b, g):
+            if g == 0:
+                vg = prep.tile([P, 2, HK * D, 4], BF16, tag="vg", align_bytes=64)
+                vg_t[b] = vg
+            nc.vector.tensor_copy(
+                out=vg_t[b][:, g, :, :].rearrange("p (c i) t -> p c t i", i=4),
+                in_=vraw_t[b][:, 4 * g : 4 * g + 4, :].rearrange("p t (c i) -> p c t i", i=4),
             )
 
         def prep_v_quant(b):
@@ -332,7 +329,8 @@ def tile_radixattention_t_kernel(tc, q, k, v, k_cache, v_cache, out):
         for first in (prep_k(0, 0, True), prep_q(0, False), prep_k(0, 1, True)):
             run(first[0])
             first[1]()
-        prep_v_group(0)
+        prep_v_group(0, 0)
+        prep_v_group(0, 1)
         prep_v_quant(0)
 
         waiting = []
@@ -384,7 +382,9 @@ def tile_radixattention_t_kernel(tc, q, k, v, k_cache, v_cache, out):
                 late()
             if prepare and i == 0 and nxt + 2 < B:
                 load(nxt + 2)
-            if prepare and i == 1:
-                prep_v_group(nxt)
+            if prepare and i == 2:
+                prep_v_group(nxt, 0)
+            if prepare and i == 4:
+                prep_v_group(nxt, 1)
             if prepare and i == 6:
                 prep_v_quant(nxt)

@@ -1,9 +1,7 @@
 from contextlib import ExitStack
 import math
 
-import concourse.bass as bass
 import concourse.mybir as mybir
-import concourse.tile as tile
 from concourse.masks import make_identity
 
 FP8X4 = mybir.dt.float8_e4m3fn_x4
@@ -13,7 +11,6 @@ U32 = mybir.dt.uint32
 U8 = mybir.dt.uint8
 ALU = mybir.AluOpType
 ACTF = mybir.ActivationFunctionType
-AX = mybir.AxisListType
 
 B, E, PRE, H, HK, D = 16, 256, 768, 4, 2, 128
 S = PRE + E
@@ -23,20 +20,19 @@ NEG = -1.0e30
 FLOPS = 2 * 2 * B * H * E * S * D
 
 NU = B * 8
-C_ON_VECTOR = (6,)
-PREP_ON_VECTOR = (True, True, True)
-MANUAL = True
+PREP_ON_VECTOR = (True, False, False)
 
 
 def tile_radixattention_t_kernel(tc, q, k, v, k_cache, v_cache, out):
     nc = tc.nc
     with ExitStack() as ctx:
-        if MANUAL:
-            ctx.enter_context(tc.manual_schedule())
+        ctx.enter_context(tc.manual_schedule())
         const = ctx.enter_context(tc.tile_pool(name="const", bufs=1))
         raw = ctx.enter_context(tc.tile_pool(name="raw", bufs=4))
         prep = ctx.enter_context(tc.tile_pool(name="prep", bufs=2))
         work = ctx.enter_context(tc.tile_pool(name="work", bufs=4))
+        one_buf = ctx.enter_context(tc.tile_pool(name="one_buf", bufs=1))
+        two_buf = ctx.enter_context(tc.tile_pool(name="two_buf", bufs=2))
         small = ctx.enter_context(tc.tile_pool(name="small", bufs=6))
         ps_s = ctx.enter_context(tc.psum_pool(name="ps_s", bufs=4))
         ps_t = ctx.enter_context(tc.psum_pool(name="ps_t", bufs=2))
@@ -81,11 +77,13 @@ def tile_radixattention_t_kernel(tc, q, k, v, k_cache, v_cache, out):
         )
         mask = const.tile([P, P], BF16, name="mask")
         nc.vector.tensor_copy(out=mask[:], in_=mask32[:])
-        ez = []
+        plz = []
         for i in range(3):
-            ezi = const.tile([P, S], BF16, name="ez%d" % i)
-            nc.vector.memset(ezi[:, S - P : S], 0.0)
-            ez.append(ezi)
+            plzi = const.tile([P, S], BF16, name="plz%d" % i)
+            nc.vector.memset(plzi[:, S - P : S], 0.0)
+            plz.append(plzi)
+        ez = const.tile([P, S], BF16, name="ez")
+        nc.vector.memset(ez[:, S - P : S], 0.0)
         warm = const.tile([P, 1], F32, name="warm")
         nc.vector.memset(warm[:], 0.0)
         warm2 = const.tile([P, 1], F32, name="warm2")
@@ -128,63 +126,61 @@ def tile_radixattention_t_kernel(tc, q, k, v, k_cache, v_cache, out):
                 on_vector, qt[:].rearrange("p i c -> p (i c)"), tp[:]
             )
 
-        def prep_v_group(b, g):
-            if g == 0:
-                vg = prep.tile([P, 2, HK * D, 4], BF16, tag="vg", align_bytes=64)
-                vg_t[b] = vg
-            nc.vector.tensor_copy(
-                out=vg_t[b][:, g, :, :].rearrange("p (c i) t -> p c t i", i=4),
-                in_=vraw_t[b][:, 4 * g : 4 * g + 4, :].rearrange("p t (c i) -> p c t i", i=4),
-            )
-
-        def prep_v_quant(b):
+        def prep_v(b):
+            vg = prep.tile([P, 2, HK * D, 4], BF16, tag="vg", align_bytes=64)
+            for g in range(2):
+                nc.vector.tensor_copy(
+                    out=vg[:, g, :, :].rearrange("p (c i) t -> p c t i", i=4),
+                    in_=vraw_t[b][:, 4 * g : 4 * g + 4, :].rearrange("p t (c i) -> p c t i", i=4),
+                )
             vcod = prep.tile([P, 2 * HK * D], U32, tag="vcod", align_bytes=64)
             vsc = prep.tile([P, 2 * HK * D], U8, tag="vsc", align_bytes=64)
             vcod_t[b], vsc_t[b] = vcod, vsc
             nc.vector.quantize_mx(
                 out=vcod[:].bitcast(FP8X4),
                 scales=vsc[:],
-                in_=vg_t[b][:].rearrange("p g x t -> p (g x t)"),
+                in_=vg[:].rearrange("p g x t -> p (g x t)"),
             )
 
         st = {}
+        gr = {}
 
         def unit(u):
             return u // 8, (u % 8) // 4, u % 4
 
         def stage_s_a(u):
             b, qb, h = unit(u)
-            hk = h // 2
-            qt = qt_t[b][:, qb * 4 + h, :]
-            kt = kt_t[b]
             s_a = ps_s.tile([P, 512], F32, tag="s")
-            nc.tensor.matmul(out=s_a[:], lhsT=qt, rhs=kt[:, hk, 0:512], start=True, stop=True)
-            st[u] = {"s_a": s_a}
+            nc.tensor.matmul(
+                out=s_a[:],
+                lhsT=qt_t[b][:, qb * 4 + h, :],
+                rhs=kt_t[b][:, h // 2, 0:512],
+                start=True,
+                stop=True,
+            )
+            st[u] = {"s_a": s_a, "nb": 384 + qb * P}
 
         def stage_s_b(u):
             b, qb, h = unit(u)
-            hk = h // 2
-            qt = qt_t[b][:, qb * 4 + h, :]
-            kt = kt_t[b]
             s_b = ps_s.tile([P, 512], F32, tag="s")
-            nfree = 256 + qb * P
+            nfree = st[u]["nb"] - P
             nc.tensor.matmul(
-                out=s_b[:, 0:nfree], lhsT=qt, rhs=kt[:, hk, 512 : 512 + nfree], start=True, stop=True
+                out=s_b[:, 0:nfree],
+                lhsT=qt_t[b][:, qb * 4 + h, :],
+                rhs=kt_t[b][:, h // 2, 512 : 512 + nfree],
+                start=True,
+                stop=True,
             )
             st[u]["s_b"] = s_b
-            st[u]["nb"] = nfree + P
 
         def stage_s_d(u):
             b, qb, h = unit(u)
-            hk = h // 2
-            qt = qt_t[b][:, qb * 4 + h, :]
-            kt = kt_t[b]
             s_b = st[u]["s_b"]
             nfree = st[u]["nb"] - P
             nc.tensor.matmul(
                 out=s_b[:, nfree : nfree + P],
-                lhsT=qt,
-                rhs=kt[:, hk, 512 + nfree : 512 + nfree + P],
+                lhsT=qt_t[b][:, qb * 4 + h, :],
+                rhs=kt_t[b][:, h // 2, 512 + nfree : 512 + nfree + P],
                 start=True,
                 stop=False,
             )
@@ -221,17 +217,14 @@ def tile_radixattention_t_kernel(tc, q, k, v, k_cache, v_cache, out):
             )
             d["bias"] = bias
 
-        sums = {}
-
         def stage_e(u):
             b, qb, h = unit(u)
             d = st[u]
             if h == 0:
                 ssum = small.tile([P, 4], F32, tag="ssum")
-                sums[u // 4] = ssum
-            ssum = sums[u // 4]
-            if qb == 0:
-                e = ez[(b * 4 + h) % 3]
+                gr[u // 4] = {"ssum": ssum}
+            if qb == 0 and h == 3:
+                e = ez
             else:
                 e = work.tile([P, S], BF16, tag="e")
             n = 512 + d["nb"]
@@ -241,11 +234,12 @@ def tile_radixattention_t_kernel(tc, q, k, v, k_cache, v_cache, out):
                 func=ACTF.Exp,
                 bias=d["bias"][:],
                 scale=-1.0,
-                accum_out=ssum[:, h : h + 1],
+                accum_out=gr[u // 4]["ssum"][:, h : h + 1],
             )
             d["e"] = e
 
         def stage_t(u):
+            b, qb, h = unit(u)
             d = st[u]
             tp = ps_t.tile([P, S], BF16, tag="t")
             d["tp"] = tp
@@ -257,66 +251,85 @@ def tile_radixattention_t_kernel(tc, q, k, v, k_cache, v_cache, out):
                     identity=ident[:],
                 )
 
-            return [one(j) for j in range(8)]
+            return [one(j) for j in range(8 if h == 3 else 4 + d["nb"] // P)]
 
         def stage_c(u):
-            d = st[u]
-            gq = work.tile([P, 2, P, 4], BF16, tag="gq", align_bytes=64)
-            copy_out(
-                (u % 8) in C_ON_VECTOR,
-                gq[:],
-                d["tp"][:].rearrange("p (g t c) -> p g c t", g=2, t=4),
-            )
-            d["gq"] = gq
-
-        def stage_q(u):
-            d = st[u]
-            ecod = work.tile([P, 2 * P], U32, tag="ecod", align_bytes=64)
-            esc = work.tile([P, 2 * P], U8, tag="esc", align_bytes=64)
-            nc.vector.quantize_mx(
-                out=ecod[:].bitcast(FP8X4),
-                scales=esc[:],
-                in_=d["gq"][:].rearrange("p g c t -> p (g c t)"),
-            )
-            d["ecod"], d["esc"] = ecod, esc
-
-        outs = {}
-
-        def stage_x(u):
             b, qb, h = unit(u)
-            hk = h // 2
+            d = st[u]
+            if h == 3:
+                nc.scalar.copy(
+                    out=gr[u // 4]["gq"][:, 3, :, :, :],
+                    in_=d["tp"][:].rearrange("p (g t c) -> p g c t", g=2, t=4),
+                )
+            else:
+                if qb == 0:
+                    pl = plz[h]
+                else:
+                    pl = work.tile([P, S], BF16, tag="pl")
+                n = 512 + d["nb"]
+                nc.scalar.copy(out=pl[:, 0:n], in_=d["tp"][:, 0:n])
+                d["pl"] = pl
+
+        def stage_g(u):
+            b, qb, h = unit(u)
             d = st[u]
             if h == 0:
-                o_ps = ps_o.tile([P, H * D], F32, tag="o")
-                outs[u // 4] = o_ps
-            o_ps = outs[u // 4]
-            for g in range(2):
-                vcols = slice((g * HK + hk) * D, (g * HK + hk + 1) * D)
-                nc.tensor.matmul_mx(
-                    out=o_ps[:, h * D : (h + 1) * D],
-                    lhsT=d["ecod"][:, g * P : (g + 1) * P].bitcast(FP8X4),
-                    lhsT_scale=d["esc"][:, g * P : (g + 1) * P],
-                    rhs=vcod_t[b][:, vcols].bitcast(FP8X4),
-                    rhs_scale=vsc_t[b][:, vcols],
-                    start=(g == 0),
-                    stop=(g == 1),
+                gq = one_buf.tile([P, 4, 2, P, 4], BF16, tag="gq", align_bytes=64)
+                gr[u // 4]["gq"] = gq
+            if h < 3:
+                nc.gpsimd.tensor_scalar(
+                    out=gr[u // 4]["gq"][:, h, :, :, :],
+                    in0=d["pl"][:].rearrange("p (g t c) -> p g c t", g=2, t=4),
+                    scalar1=1.0,
+                    scalar2=0.0,
+                    op0=ALU.mult,
+                    op1=ALU.add,
                 )
 
-        rinvs = {}
+        def stage_q(su, half):
+            d = gr[su]
+            if half == 1:
+                ecod = two_buf.tile([P, 8 * P], U32, tag="ecod", align_bytes=64)
+                esc = two_buf.tile([P, 8 * P], U8, tag="esc", align_bytes=64)
+                d["ecod"], d["esc"] = ecod, esc
+            cols = slice(half * 4 * P, (half + 1) * 4 * P)
+            nc.vector.quantize_mx(
+                out=d["ecod"][:, cols].bitcast(FP8X4),
+                scales=d["esc"][:, cols],
+                in_=d["gq"][:, 2 * half : 2 * half + 2, :, :, :].rearrange("p u g c t -> p (u g c t)"),
+            )
+
+        def stage_x(su):
+            b = su // 2
+            d = gr[su]
+            o_ps = ps_o.tile([P, H * D], F32, tag="o")
+            d["o_ps"] = o_ps
+            for h in range(H):
+                for g in range(2):
+                    vcols = slice((g * HK + h // 2) * D, (g * HK + h // 2 + 1) * D)
+                    ecols = slice((h * 2 + g) * P, (h * 2 + g + 1) * P)
+                    nc.tensor.matmul_mx(
+                        out=o_ps[:, h * D : (h + 1) * D],
+                        lhsT=d["ecod"][:, ecols].bitcast(FP8X4),
+                        lhsT_scale=d["esc"][:, ecols],
+                        rhs=vcod_t[b][:, vcols].bitcast(FP8X4),
+                        rhs_scale=vsc_t[b][:, vcols],
+                        start=(g == 0),
+                        stop=(g == 1),
+                    )
 
         def stage_r(su):
             rinv = small.tile([P, 4], F32, tag="rinv")
-            nc.vector.reciprocal(out=rinv[:], in_=sums[su][:])
-            rinvs[su] = rinv
+            nc.vector.reciprocal(out=rinv[:], in_=gr[su]["ssum"][:])
+            gr[su]["rinv"] = rinv
 
         def stage_n(su):
             b, qb = su // 2, su % 2
-            rinv = rinvs[su]
             o_sb = work.tile([P, H, D], F32, tag="o_sb")
             nc.vector.tensor_tensor(
                 out=o_sb[:],
-                in0=outs[su][:].rearrange("p (h d) -> p h d", h=H),
-                in1=rinv[:].unsqueeze(2).to_broadcast([P, H, D]),
+                in0=gr[su]["o_ps"][:].rearrange("p (h d) -> p h d", h=H),
+                in1=gr[su]["rinv"][:].unsqueeze(2).to_broadcast([P, H, D]),
                 op=ALU.mult,
             )
             r0 = b * E + qb * P
@@ -326,27 +339,36 @@ def tile_radixattention_t_kernel(tc, q, k, v, k_cache, v_cache, out):
             for call in calls:
                 call()
 
-        for first in (prep_k(0, 0, True), prep_q(0, False), prep_k(0, 1, True)):
+        def ok(u):
+            return 0 <= u < NU
+
+        for which in range(3):
+            if which == 0:
+                first = prep_k(0, 0, True)
+            elif which == 1:
+                first = prep_q(0, False)
+            else:
+                first = prep_k(0, 1, True)
             run(first[0])
             first[1]()
-        prep_v_group(0, 0)
-        prep_v_group(0, 1)
-        prep_v_quant(0)
+        prep_v(0)
 
         waiting = []
-        for step in range(-1, NU + 6):
+        for step in range(-3, NU + 9):
             nxt = step // 8 + 1
             i = step % 8
             prepare = 0 <= step < NU and nxt < B
             late = None
-            if 0 <= step - 1 < NU:
+            if ok(step - 1):
                 stage_e(step - 1)
-            if 0 <= step < NU:
-                stage_m_a(step)
-            if 0 <= step - 5 < NU and (step - 5) % 4 == 3:
-                stage_n((step - 5) // 4)
+            if ok(step + 2):
+                stage_m_a(step + 2)
+            if ok(step - 8) and (step - 8) % 4 == 0:
+                stage_n((step - 8) // 4)
+            if ok(step + 1):
+                stage_m_b(step + 1)
             tr = []
-            if 0 <= step - 2 < NU:
+            if ok(step - 2):
                 tr = stage_t(step - 2)
             if prepare and i in (0, 2, 4):
                 if i == 0:
@@ -360,31 +382,27 @@ def tile_radixattention_t_kernel(tc, q, k, v, k_cache, v_cache, out):
                 late = group[1]
             tr = tr + waiting[0:4]
             waiting = waiting[4:]
-            if 0 <= step + 1 < NU:
-                stage_s_a(step + 1)
+            if ok(step + 3):
+                stage_s_a(step + 3)
             run(tr[0:6])
-            if 0 <= step + 1 < NU:
-                stage_s_b(step + 1)
+            if ok(step + 2):
+                stage_s_b(step + 2)
             run(tr[6:])
-            if 0 <= step + 1 < NU:
-                stage_s_d(step + 1)
-            if 0 <= step - 4 < NU:
-                stage_x(step - 4)
-            if 0 <= step - 3 < NU:
-                stage_q(step - 3)
-            if 0 <= step < NU:
-                stage_m_b(step)
-            if 0 <= step - 2 < NU:
+            if ok(step + 2):
+                stage_s_d(step + 2)
+            if ok(step - 7) and (step - 7) % 4 == 0:
+                stage_x((step - 7) // 4)
+            if ok(step - 3):
+                stage_g(step - 3)
+            if ok(step - 2):
                 stage_c(step - 2)
-            if 0 <= step - 2 < NU and (step - 2) % 4 == 3:
-                stage_r((step - 2) // 4)
+            if ok(step - 6) and (step - 6) % 4 == 0:
+                stage_q((step - 6) // 4, 1)
+                if prepare and i == 6:
+                    prep_v(nxt)
+                stage_q((step - 6) // 4, 0)
+                stage_r((step - 6) // 4)
             if late is not None:
                 late()
             if prepare and i == 0 and nxt + 2 < B:
                 load(nxt + 2)
-            if prepare and i == 2:
-                prep_v_group(nxt, 0)
-            if prepare and i == 4:
-                prep_v_group(nxt, 1)
-            if prepare and i == 6:
-                prep_v_quant(nxt)

@@ -49,11 +49,11 @@ def tile_radixattention_t_kernel(tc, q, k, v, k_cache, v_cache, out):
         kt_t, qt_t, vg_t, vcod_t, vsc_t = {}, {}, {}, {}, {}
 
         def load(b):
+            qraw = raw.tile([P, 2, H * D], BF16, tag="qraw")
+            nc.sync.dma_start(out=qraw[:], in_=q_v[b])
             kraw = raw.tile([P, 8, HK * D], BF16, tag="kraw")
             nc.sync.dma_start(out=kraw[:, 0:6, :], in_=kc_v[b])
             nc.sync.dma_start(out=kraw[:, 6:8, :], in_=k_v[b])
-            qraw = raw.tile([P, 2, H * D], BF16, tag="qraw")
-            nc.sync.dma_start(out=qraw[:], in_=q_v[b])
             vraw = raw.tile([P, 8, HK * D], BF16, tag="vraw")
             nc.sync.dma_start(out=vraw[:, 0:6, :], in_=vc_v[b])
             nc.sync.dma_start(out=vraw[:, 6:8, :], in_=v_v[b])
@@ -78,12 +78,10 @@ def tile_radixattention_t_kernel(tc, q, k, v, k_cache, v_cache, out):
         mask = const.tile([P, P], BF16, name="mask")
         nc.vector.tensor_copy(out=mask[:], in_=mask32[:])
         plz = []
-        for i in range(3):
+        for i in range(4):
             plzi = const.tile([P, S], BF16, name="plz%d" % i)
             nc.vector.memset(plzi[:, S - P : S], 0.0)
             plz.append(plzi)
-        ez = const.tile([P, S], BF16, name="ez")
-        nc.vector.memset(ez[:, S - P : S], 0.0)
         warm = const.tile([P, 1], F32, name="warm")
         nc.vector.memset(warm[:], 0.0)
         warm2 = const.tile([P, 1], F32, name="warm2")
@@ -95,11 +93,11 @@ def tile_radixattention_t_kernel(tc, q, k, v, k_cache, v_cache, out):
             else:
                 nc.scalar.copy(out=dst, in_=src)
 
-        def prep_k(b, hk, on_vector):
+        def prep_k(b, hk, on_vector, pool=ps_p, tag="p"):
             if hk == 0:
                 kt = prep.tile([P, HK, S], BF16, tag="kt")
                 kt_t[b] = kt
-            tp = ps_p.tile([P, S], BF16, tag="p")
+            tp = pool.tile([P, S], BF16, tag=tag)
 
             def one(c):
                 return lambda: nc.tensor.transpose(
@@ -110,10 +108,10 @@ def tile_radixattention_t_kernel(tc, q, k, v, k_cache, v_cache, out):
 
             return [one(c) for c in range(8)], lambda: copy_out(on_vector, kt_t[b][:, hk, :], tp[:])
 
-        def prep_q(b, on_vector):
+        def prep_q(b, on_vector, pool=ps_p, tag="p"):
             qt = prep.tile([P, 8, P], BF16, tag="qt")
             qt_t[b] = qt
-            tp = ps_p.tile([P, S], BF16, tag="p")
+            tp = pool.tile([P, S], BF16, tag=tag)
 
             def one(i):
                 return lambda: nc.tensor.transpose(
@@ -223,10 +221,7 @@ def tile_radixattention_t_kernel(tc, q, k, v, k_cache, v_cache, out):
             if h == 0:
                 ssum = small.tile([P, 4], F32, tag="ssum")
                 gr[u // 4] = {"ssum": ssum}
-            if qb == 0 and h == 3:
-                e = ez
-            else:
-                e = work.tile([P, S], BF16, tag="e")
+            e = work.tile([P, S], BF16, tag="e")
             n = 512 + d["nb"]
             nc.scalar.activation(
                 out=e[:, 0:n],
@@ -251,12 +246,12 @@ def tile_radixattention_t_kernel(tc, q, k, v, k_cache, v_cache, out):
                     identity=ident[:],
                 )
 
-            return [one(j) for j in range(8 if h == 3 else 4 + d["nb"] // P)]
+            return [one(j) for j in range(4 + d["nb"] // P)]
 
         def stage_c(u):
             b, qb, h = unit(u)
             d = st[u]
-            if h == 3:
+            if qb == 1 and h == 3:
                 nc.scalar.copy(
                     out=gr[u // 4]["gq"][:, 3, :, :, :],
                     in_=d["tp"][:].rearrange("p (g t c) -> p g c t", g=2, t=4),
@@ -276,7 +271,7 @@ def tile_radixattention_t_kernel(tc, q, k, v, k_cache, v_cache, out):
             if h == 0:
                 gq = one_buf.tile([P, 4, 2, P, 4], BF16, tag="gq", align_bytes=64)
                 gr[u // 4]["gq"] = gq
-            if h < 3:
+            if qb == 0 or h < 3:
                 nc.gpsimd.tensor_scalar(
                     out=gr[u // 4]["gq"][:, h, :, :, :],
                     in0=d["pl"][:].rearrange("p (g t c) -> p g c t", g=2, t=4),
@@ -342,31 +337,41 @@ def tile_radixattention_t_kernel(tc, q, k, v, k_cache, v_cache, out):
         def ok(u):
             return 0 <= u < NU
 
-        for which in range(3):
-            if which == 0:
-                first = prep_k(0, 0, True)
-            elif which == 1:
-                first = prep_q(0, False)
-            else:
-                first = prep_k(0, 1, True)
-            run(first[0])
-            first[1]()
-        prep_v(0)
+        first = prep_q(0, False, ps_t, "t")
+        run(first[0])
+        first[1]()
+        first = prep_k(0, 0, True, ps_t, "t")
+        run(first[0])
+        first[1]()
+        group = prep_k(0, 1, False)
+        waiting = group[0]
 
-        waiting = []
-        for step in range(-3, NU + 9):
+        for step in range(-3, NU + 10):
             nxt = step // 8 + 1
             i = step % 8
             prepare = 0 <= step < NU and nxt < B
-            late = None
             if ok(step - 1):
                 stage_e(step - 1)
             if ok(step + 2):
                 stage_m_a(step + 2)
-            if ok(step - 8) and (step - 8) % 4 == 0:
+            if i == 1 and ok(step - 9):
+                stage_n((step - 9) // 4)
+            if i == 4 and ok(step - 8):
                 stage_n((step - 8) // 4)
             if ok(step + 1):
                 stage_m_b(step + 1)
+            if step == 0:
+                prep_v(0)
+            if i == 7 and ok(step - 7):
+                stage_q((step - 7) // 4, 1)
+                stage_q((step - 7) // 4, 0)
+                stage_r((step - 7) // 4)
+            if i == 2 and ok(step - 6):
+                stage_q((step - 6) // 4, 1)
+                if step // 8 < B:
+                    prep_v(step // 8)
+                stage_q((step - 6) // 4, 0)
+                stage_r((step - 6) // 4)
             tr = []
             if ok(step - 2):
                 tr = stage_t(step - 2)
@@ -378,8 +383,7 @@ def tile_radixattention_t_kernel(tc, q, k, v, k_cache, v_cache, out):
                 else:
                     group = prep_k(nxt, 1, PREP_ON_VECTOR[2])
                 waiting = group[0]
-            if prepare and i in (1, 3, 5):
-                late = group[1]
+            late = len(waiting) > 0 and len(waiting) <= 4
             tr = tr + waiting[0:4]
             waiting = waiting[4:]
             if ok(step + 3):
@@ -390,19 +394,15 @@ def tile_radixattention_t_kernel(tc, q, k, v, k_cache, v_cache, out):
             run(tr[6:])
             if ok(step + 2):
                 stage_s_d(step + 2)
-            if ok(step - 7) and (step - 7) % 4 == 0:
+            if i == 0 and ok(step - 8):
+                stage_x((step - 8) // 4)
+            if i == 3 and ok(step - 7):
                 stage_x((step - 7) // 4)
             if ok(step - 3):
                 stage_g(step - 3)
             if ok(step - 2):
                 stage_c(step - 2)
-            if ok(step - 6) and (step - 6) % 4 == 0:
-                stage_q((step - 6) // 4, 1)
-                if prepare and i == 6:
-                    prep_v(nxt)
-                stage_q((step - 6) // 4, 0)
-                stage_r((step - 6) // 4)
-            if late is not None:
-                late()
+            if late:
+                group[1]()
             if prepare and i == 0 and nxt + 2 < B:
                 load(nxt + 2)

@@ -49,11 +49,11 @@ def tile_radixattention_t_kernel(tc, q, k, v, k_cache, v_cache, out):
         kt_t, qt_t, vg_t, vcod_t, vsc_t = {}, {}, {}, {}, {}
 
         def load(b):
-            qraw = raw.tile([P, 2, H * D], BF16, tag="qraw")
-            nc.sync.dma_start(out=qraw[:], in_=q_v[b])
             kraw = raw.tile([P, 8, HK * D], BF16, tag="kraw")
             nc.sync.dma_start(out=kraw[:, 0:6, :], in_=kc_v[b])
             nc.sync.dma_start(out=kraw[:, 6:8, :], in_=k_v[b])
+            qraw = raw.tile([P, 2, H * D], BF16, tag="qraw")
+            nc.sync.dma_start(out=qraw[:], in_=q_v[b])
             vraw = raw.tile([P, 8, HK * D], BF16, tag="vraw")
             nc.sync.dma_start(out=vraw[:, 0:6, :], in_=vc_v[b])
             nc.sync.dma_start(out=vraw[:, 6:8, :], in_=v_v[b])
@@ -78,10 +78,12 @@ def tile_radixattention_t_kernel(tc, q, k, v, k_cache, v_cache, out):
         mask = const.tile([P, P], BF16, name="mask")
         nc.vector.tensor_copy(out=mask[:], in_=mask32[:])
         plz = []
-        for i in range(4):
+        for i in range(3):
             plzi = const.tile([P, S], BF16, name="plz%d" % i)
             nc.vector.memset(plzi[:, S - P : S], 0.0)
             plz.append(plzi)
+        ez = const.tile([P, S], BF16, name="ez")
+        nc.vector.memset(ez[:, S - P : S], 0.0)
         warm = const.tile([P, 1], F32, name="warm")
         nc.vector.memset(warm[:], 0.0)
         warm2 = const.tile([P, 1], F32, name="warm2")
@@ -93,11 +95,11 @@ def tile_radixattention_t_kernel(tc, q, k, v, k_cache, v_cache, out):
             else:
                 nc.scalar.copy(out=dst, in_=src)
 
-        def prep_k(b, hk, on_vector, pool=ps_p, tag="p"):
+        def prep_k(b, hk, on_vector):
             if hk == 0:
                 kt = prep.tile([P, HK, S], BF16, tag="kt")
                 kt_t[b] = kt
-            tp = pool.tile([P, S], BF16, tag=tag)
+            tp = ps_p.tile([P, S], BF16, tag="p")
 
             def one(c):
                 return lambda: nc.tensor.transpose(
@@ -108,10 +110,10 @@ def tile_radixattention_t_kernel(tc, q, k, v, k_cache, v_cache, out):
 
             return [one(c) for c in range(8)], lambda: copy_out(on_vector, kt_t[b][:, hk, :], tp[:])
 
-        def prep_q(b, on_vector, pool=ps_p, tag="p"):
+        def prep_q(b, on_vector):
             qt = prep.tile([P, 8, P], BF16, tag="qt")
             qt_t[b] = qt
-            tp = pool.tile([P, S], BF16, tag=tag)
+            tp = ps_p.tile([P, S], BF16, tag="p")
 
             def one(i):
                 return lambda: nc.tensor.transpose(
@@ -142,6 +144,7 @@ def tile_radixattention_t_kernel(tc, q, k, v, k_cache, v_cache, out):
 
         st = {}
         gr = {}
+        o_t = {}
 
         def unit(u):
             return u // 8, (u % 8) // 4, u % 4
@@ -221,7 +224,10 @@ def tile_radixattention_t_kernel(tc, q, k, v, k_cache, v_cache, out):
             if h == 0:
                 ssum = small.tile([P, 4], F32, tag="ssum")
                 gr[u // 4] = {"ssum": ssum}
-            e = work.tile([P, S], BF16, tag="e")
+            if qb == 0 and h == 3:
+                e = ez
+            else:
+                e = work.tile([P, S], BF16, tag="e")
             n = 512 + d["nb"]
             nc.scalar.activation(
                 out=e[:, 0:n],
@@ -246,12 +252,12 @@ def tile_radixattention_t_kernel(tc, q, k, v, k_cache, v_cache, out):
                     identity=ident[:],
                 )
 
-            return [one(j) for j in range(4 + d["nb"] // P)]
+            return [one(j) for j in range(8 if h == 3 else 4 + d["nb"] // P)]
 
         def stage_c(u):
             b, qb, h = unit(u)
             d = st[u]
-            if qb == 1 and h == 3:
+            if h == 3:
                 nc.scalar.copy(
                     out=gr[u // 4]["gq"][:, 3, :, :, :],
                     in_=d["tp"][:].rearrange("p (g t c) -> p g c t", g=2, t=4),
@@ -271,7 +277,7 @@ def tile_radixattention_t_kernel(tc, q, k, v, k_cache, v_cache, out):
             if h == 0:
                 gq = one_buf.tile([P, 4, 2, P, 4], BF16, tag="gq", align_bytes=64)
                 gr[u // 4]["gq"] = gq
-            if qb == 0 or h < 3:
+            if h < 3:
                 nc.gpsimd.tensor_scalar(
                     out=gr[u // 4]["gq"][:, h, :, :, :],
                     in0=d["pl"][:].rearrange("p (g t c) -> p g c t", g=2, t=4),
@@ -294,10 +300,27 @@ def tile_radixattention_t_kernel(tc, q, k, v, k_cache, v_cache, out):
                 in_=d["gq"][:, 2 * half : 2 * half + 2, :, :, :].rearrange("p u g c t -> p (u g c t)"),
             )
 
+        def filler(su, b):
+            if su not in o_t:
+                o_ps = ps_o.tile([P, H * D], F32, tag="o")
+                o_t[su] = o_ps
+            nc.tensor.matmul_mx(
+                out=o_t[su][:],
+                lhsT=vcod_t[b][:, 0:P].bitcast(FP8X4),
+                lhsT_scale=vsc_t[b][:, 0:P],
+                rhs=vcod_t[b][:].bitcast(FP8X4),
+                rhs_scale=vsc_t[b][:],
+                start=True,
+                stop=True,
+            )
+
         def stage_x(su):
             b = su // 2
             d = gr[su]
-            o_ps = ps_o.tile([P, H * D], F32, tag="o")
+            if su not in o_t:
+                o_ps = ps_o.tile([P, H * D], F32, tag="o")
+                o_t[su] = o_ps
+            o_ps = o_t[su]
             d["o_ps"] = o_ps
             for h in range(H):
                 for g in range(2):
@@ -337,41 +360,31 @@ def tile_radixattention_t_kernel(tc, q, k, v, k_cache, v_cache, out):
         def ok(u):
             return 0 <= u < NU
 
-        first = prep_q(0, False, ps_t, "t")
-        run(first[0])
-        first[1]()
-        first = prep_k(0, 0, True, ps_t, "t")
-        run(first[0])
-        first[1]()
-        group = prep_k(0, 1, False)
-        waiting = group[0]
+        for which in range(3):
+            if which == 0:
+                first = prep_k(0, 0, True)
+            elif which == 1:
+                first = prep_q(0, False)
+            else:
+                first = prep_k(0, 1, True)
+            run(first[0])
+            first[1]()
+        prep_v(0)
 
-        for step in range(-3, NU + 10):
+        waiting = []
+        for step in range(-3, NU + 9):
             nxt = step // 8 + 1
             i = step % 8
             prepare = 0 <= step < NU and nxt < B
+            late = None
             if ok(step - 1):
                 stage_e(step - 1)
             if ok(step + 2):
                 stage_m_a(step + 2)
-            if i == 1 and ok(step - 9):
-                stage_n((step - 9) // 4)
-            if i == 4 and ok(step - 8):
+            if ok(step - 8) and (step - 8) % 4 == 0:
                 stage_n((step - 8) // 4)
             if ok(step + 1):
                 stage_m_b(step + 1)
-            if step == 0:
-                prep_v(0)
-            if i == 7 and ok(step - 7):
-                stage_q((step - 7) // 4, 1)
-                stage_q((step - 7) // 4, 0)
-                stage_r((step - 7) // 4)
-            if i == 2 and ok(step - 6):
-                stage_q((step - 6) // 4, 1)
-                if step // 8 < B:
-                    prep_v(step // 8)
-                stage_q((step - 6) // 4, 0)
-                stage_r((step - 6) // 4)
             tr = []
             if ok(step - 2):
                 tr = stage_t(step - 2)
@@ -383,7 +396,8 @@ def tile_radixattention_t_kernel(tc, q, k, v, k_cache, v_cache, out):
                 else:
                     group = prep_k(nxt, 1, PREP_ON_VECTOR[2])
                 waiting = group[0]
-            late = len(waiting) > 0 and len(waiting) <= 4
+            if prepare and i in (1, 3, 5):
+                late = group[1]
             tr = tr + waiting[0:4]
             waiting = waiting[4:]
             if ok(step + 3):
@@ -394,15 +408,21 @@ def tile_radixattention_t_kernel(tc, q, k, v, k_cache, v_cache, out):
             run(tr[6:])
             if ok(step + 2):
                 stage_s_d(step + 2)
-            if i == 0 and ok(step - 8):
-                stage_x((step - 8) // 4)
-            if i == 3 and ok(step - 7):
+            if ok(step - 7) and (step - 7) % 4 == 0:
                 stage_x((step - 7) // 4)
+            elif 0 <= step < NU + 3:
+                filler(max(step - 4, 0) // 4, min(max(step - 4, 0) // 8, B - 1))
             if ok(step - 3):
                 stage_g(step - 3)
             if ok(step - 2):
                 stage_c(step - 2)
-            if late:
-                group[1]()
+            if ok(step - 6) and (step - 6) % 4 == 0:
+                stage_q((step - 6) // 4, 1)
+                if prepare and i == 6:
+                    prep_v(nxt)
+                stage_q((step - 6) // 4, 0)
+                stage_r((step - 6) // 4)
+            if late is not None:
+                late()
             if prepare and i == 0 and nxt + 2 < B:
                 load(nxt + 2)

@@ -20,7 +20,6 @@ NEG = -1.0e30
 FLOPS = 2 * 2 * B * H * E * S * D
 
 NU = B * 8
-PREP_ON_VECTOR = (True, False, False)
 
 
 def tile_radixattention_t_kernel(tc, q, k, v, k_cache, v_cache, out):
@@ -49,11 +48,11 @@ def tile_radixattention_t_kernel(tc, q, k, v, k_cache, v_cache, out):
         kt_t, qt_t, vg_t, vcod_t, vsc_t = {}, {}, {}, {}, {}
 
         def load(b):
+            qraw = raw.tile([P, 2, H * D], BF16, tag="qraw")
+            nc.sync.dma_start(out=qraw[:], in_=q_v[b])
             kraw = raw.tile([P, 8, HK * D], BF16, tag="kraw")
             nc.sync.dma_start(out=kraw[:, 0:6, :], in_=kc_v[b])
             nc.sync.dma_start(out=kraw[:, 6:8, :], in_=k_v[b])
-            qraw = raw.tile([P, 2, H * D], BF16, tag="qraw")
-            nc.sync.dma_start(out=qraw[:], in_=q_v[b])
             vraw = raw.tile([P, 8, HK * D], BF16, tag="vraw")
             nc.sync.dma_start(out=vraw[:, 0:6, :], in_=vc_v[b])
             nc.sync.dma_start(out=vraw[:, 6:8, :], in_=v_v[b])
@@ -95,11 +94,11 @@ def tile_radixattention_t_kernel(tc, q, k, v, k_cache, v_cache, out):
             else:
                 nc.scalar.copy(out=dst, in_=src)
 
-        def prep_k(b, hk, on_vector):
+        def prep_k(b, hk, on_vector, pool=ps_p, tag="p"):
             if hk == 0:
                 kt = prep.tile([P, HK, S], BF16, tag="kt")
                 kt_t[b] = kt
-            tp = ps_p.tile([P, S], BF16, tag="p")
+            tp = pool.tile([P, S], BF16, tag=tag)
 
             def one(c):
                 return lambda: nc.tensor.transpose(
@@ -110,10 +109,10 @@ def tile_radixattention_t_kernel(tc, q, k, v, k_cache, v_cache, out):
 
             return [one(c) for c in range(8)], lambda: copy_out(on_vector, kt_t[b][:, hk, :], tp[:])
 
-        def prep_q(b, on_vector):
+        def prep_q(b, on_vector, pool=ps_p, tag="p"):
             qt = prep.tile([P, 8, P], BF16, tag="qt")
             qt_t[b] = qt
-            tp = ps_p.tile([P, S], BF16, tag="p")
+            tp = pool.tile([P, S], BF16, tag=tag)
 
             def one(i):
                 return lambda: nc.tensor.transpose(
@@ -144,10 +143,12 @@ def tile_radixattention_t_kernel(tc, q, k, v, k_cache, v_cache, out):
 
         st = {}
         gr = {}
-        o_t = {}
 
         def unit(u):
             return u // 8, (u % 8) // 4, u % 4
+
+        def permuted_copy(u):
+            return u % 4 == 3 or u == NU - 2
 
         def stage_s_a(u):
             b, qb, h = unit(u)
@@ -257,10 +258,11 @@ def tile_radixattention_t_kernel(tc, q, k, v, k_cache, v_cache, out):
         def stage_c(u):
             b, qb, h = unit(u)
             d = st[u]
-            if h == 3:
-                nc.scalar.copy(
-                    out=gr[u // 4]["gq"][:, 3, :, :, :],
-                    in_=d["tp"][:].rearrange("p (g t c) -> p g c t", g=2, t=4),
+            if permuted_copy(u):
+                copy_out(
+                    u == NU - 1,
+                    gr[u // 4]["gq"][:, h, :, :, :],
+                    d["tp"][:].rearrange("p (g t c) -> p g c t", g=2, t=4),
                 )
             else:
                 if qb == 0:
@@ -277,7 +279,7 @@ def tile_radixattention_t_kernel(tc, q, k, v, k_cache, v_cache, out):
             if h == 0:
                 gq = one_buf.tile([P, 4, 2, P, 4], BF16, tag="gq", align_bytes=64)
                 gr[u // 4]["gq"] = gq
-            if h < 3:
+            if not permuted_copy(u):
                 nc.gpsimd.tensor_scalar(
                     out=gr[u // 4]["gq"][:, h, :, :, :],
                     in0=d["pl"][:].rearrange("p (g t c) -> p g c t", g=2, t=4),
@@ -289,7 +291,7 @@ def tile_radixattention_t_kernel(tc, q, k, v, k_cache, v_cache, out):
 
         def stage_q(su, half):
             d = gr[su]
-            if half == 1:
+            if "ecod" not in d:
                 ecod = two_buf.tile([P, 8 * P], U32, tag="ecod", align_bytes=64)
                 esc = two_buf.tile([P, 8 * P], U8, tag="esc", align_bytes=64)
                 d["ecod"], d["esc"] = ecod, esc
@@ -300,27 +302,10 @@ def tile_radixattention_t_kernel(tc, q, k, v, k_cache, v_cache, out):
                 in_=d["gq"][:, 2 * half : 2 * half + 2, :, :, :].rearrange("p u g c t -> p (u g c t)"),
             )
 
-        def filler(su, b):
-            if su not in o_t:
-                o_ps = ps_o.tile([P, H * D], F32, tag="o")
-                o_t[su] = o_ps
-            nc.tensor.matmul_mx(
-                out=o_t[su][:],
-                lhsT=vcod_t[b][:, 0:P].bitcast(FP8X4),
-                lhsT_scale=vsc_t[b][:, 0:P],
-                rhs=vcod_t[b][:].bitcast(FP8X4),
-                rhs_scale=vsc_t[b][:],
-                start=True,
-                stop=True,
-            )
-
         def stage_x(su):
             b = su // 2
             d = gr[su]
-            if su not in o_t:
-                o_ps = ps_o.tile([P, H * D], F32, tag="o")
-                o_t[su] = o_ps
-            o_ps = o_t[su]
+            o_ps = ps_o.tile([P, H * D], F32, tag="o")
             d["o_ps"] = o_ps
             for h in range(H):
                 for g in range(2):
@@ -360,23 +345,19 @@ def tile_radixattention_t_kernel(tc, q, k, v, k_cache, v_cache, out):
         def ok(u):
             return 0 <= u < NU
 
-        for which in range(3):
-            if which == 0:
-                first = prep_k(0, 0, True)
-            elif which == 1:
-                first = prep_q(0, False)
-            else:
-                first = prep_k(0, 1, True)
-            run(first[0])
-            first[1]()
-        prep_v(0)
+        first = prep_q(0, False, ps_t, "t")
+        run(first[0])
+        first[1]()
+        first = prep_k(0, 0, True, ps_t, "t")
+        run(first[0])
+        first[1]()
+        group = prep_k(0, 1, False)
+        waiting = group[0]
 
-        waiting = []
         for step in range(-3, NU + 9):
             nxt = step // 8 + 1
             i = step % 8
             prepare = 0 <= step < NU and nxt < B
-            late = None
             if ok(step - 1):
                 stage_e(step - 1)
             if ok(step + 2):
@@ -385,19 +366,20 @@ def tile_radixattention_t_kernel(tc, q, k, v, k_cache, v_cache, out):
                 stage_n((step - 8) // 4)
             if ok(step + 1):
                 stage_m_b(step + 1)
+            if step == 0:
+                prep_v(0)
             tr = []
             if ok(step - 2):
                 tr = stage_t(step - 2)
             if prepare and i in (0, 2, 4):
                 if i == 0:
-                    group = prep_k(nxt, 0, PREP_ON_VECTOR[0])
+                    group = prep_k(nxt, 0, True)
                 elif i == 2:
-                    group = prep_q(nxt, PREP_ON_VECTOR[1])
+                    group = prep_q(nxt, nxt % 2 == 1)
                 else:
-                    group = prep_k(nxt, 1, PREP_ON_VECTOR[2])
+                    group = prep_k(nxt, 1, False)
                 waiting = group[0]
-            if prepare and i in (1, 3, 5):
-                late = group[1]
+            late = 0 < len(waiting) <= 4
             tr = tr + waiting[0:4]
             waiting = waiting[4:]
             if ok(step + 3):
@@ -410,19 +392,21 @@ def tile_radixattention_t_kernel(tc, q, k, v, k_cache, v_cache, out):
                 stage_s_d(step + 2)
             if ok(step - 7) and (step - 7) % 4 == 0:
                 stage_x((step - 7) // 4)
-            elif 0 <= step < NU + 3:
-                filler(max(step - 4, 0) // 4, min(max(step - 4, 0) // 8, B - 1))
             if ok(step - 3):
                 stage_g(step - 3)
+            if step == NU + 1:
+                stage_q(NU // 4 - 1, 0)
             if ok(step - 2):
                 stage_c(step - 2)
             if ok(step - 6) and (step - 6) % 4 == 0:
-                stage_q((step - 6) // 4, 1)
+                su = (step - 6) // 4
+                stage_q(su, 1)
                 if prepare and i == 6:
                     prep_v(nxt)
-                stage_q((step - 6) // 4, 0)
-                stage_r((step - 6) // 4)
-            if late is not None:
-                late()
+                if su < NU // 4 - 1:
+                    stage_q(su, 0)
+                stage_r(su)
+            if late:
+                group[1]()
             if prepare and i == 0 and nxt + 2 < B:
                 load(nxt + 2)

from contextlib import ExitStack
import math

import concourse.mybir as mybir
from concourse.masks import make_identity

FP8X4 = mybir.dt.float8_e4m3fn_x4
BF16 = mybir.dt.bfloat16
F32 = mybir.dt.float32
U32 = mybir.dt.uint32
U8 = mybir.dt.uint8
ALU = mybir.AluOpType
ACTF = mybir.ActivationFunctionType

B, E, PRE, H, HK, D = 16, 256, 768, 4, 2, 128
S = PRE + E
P = 128
SCALING = 1.0 / math.sqrt(D)
NEG = -1.0e30
FLOPS = 2 * 2 * B * H * E * S * D

NU = B * 8


def tile_radixattention_t_kernel(tc, q, k, v, k_cache, v_cache, out):
    nc = tc.nc
    with ExitStack() as ctx:
        ctx.enter_context(tc.manual_schedule())
        const = ctx.enter_context(tc.tile_pool(name="const", bufs=1))
        raw = ctx.enter_context(tc.tile_pool(name="raw", bufs=4))
        prep = ctx.enter_context(tc.tile_pool(name="prep", bufs=2))
        work = ctx.enter_context(tc.tile_pool(name="work", bufs=4))
        one_buf = ctx.enter_context(tc.tile_pool(name="one_buf", bufs=1))
        two_buf = ctx.enter_context(tc.tile_pool(name="two_buf", bufs=2))
        small = ctx.enter_context(tc.tile_pool(name="small", bufs=6))
        ps_s = ctx.enter_context(tc.psum_pool(name="ps_s", bufs=4))
        ps_t = ctx.enter_context(tc.psum_pool(name="ps_t", bufs=2))
        ps_p = ctx.enter_context(tc.psum_pool(name="ps_p", bufs=1))
        ps_o = ctx.enter_context(tc.psum_pool(name="ps_o", bufs=1))

        q_v = q.rearrange("b (qb p) h d -> b p qb (h d)", p=P)
        k_v = k.rearrange("b (c p) hk d -> b p c (hk d)", p=P)
        kc_v = k_cache.rearrange("b (c p) hk d -> b p c (hk d)", p=P)
        v_v = v.rearrange("b (c p) hk d -> b p c (hk d)", p=P)
        vc_v = v_cache.rearrange("b (c p) hk d -> b p c (hk d)", p=P)

        kraw_t, qraw_t, vraw_t = {}, {}, {}
        kt_t, qt_t, vg_t, vcod_t, vsc_t = {}, {}, {}, {}, {}

        def load(b):
            qraw = raw.tile([P, 2, H * D], BF16, tag="qraw")
            nc.sync.dma_start(out=qraw[:], in_=q_v[b])
            kraw = raw.tile([P, 8, HK * D], BF16, tag="kraw")
            nc.sync.dma_start(out=kraw[:, 0:6, :], in_=kc_v[b])
            nc.sync.dma_start(out=kraw[:, 6:8, :], in_=k_v[b])
            vraw = raw.tile([P, 8, HK * D], BF16, tag="vraw")
            nc.sync.dma_start(out=vraw[:, 0:6, :], in_=vc_v[b])
            nc.sync.dma_start(out=vraw[:, 6:8, :], in_=v_v[b])
            kraw_t[b], qraw_t[b], vraw_t[b] = kraw, qraw, vraw

        for b in range(3):
            load(b)

        ident = const.tile([P, P], BF16, name="ident")
        make_identity(nc, ident[:])
        mask32 = const.tile([P, P], F32, name="mask32")
        nc.gpsimd.memset(mask32[:], 0.0)
        nc.gpsimd.affine_select(
            out=mask32[:],
            in_=mask32[:],
            compare_op=ALU.is_ge,
            fill=NEG,
            base=0,
            pattern=[[-1, P]],
            channel_multiplier=1,
        )
        mask = const.tile([P, P], BF16, name="mask")
        nc.vector.tensor_copy(out=mask[:], in_=mask32[:])
        plz = []
        for i in range(3):
            plzi = const.tile([P, S], BF16, name="plz%d" % i)
            nc.vector.memset(plzi[:, S - P : S], 0.0)
            plz.append(plzi)
        ez = const.tile([P, S], BF16, name="ez")
        nc.vector.memset(ez[:, S - P : S], 0.0)
        warm = const.tile([P, 1], F32, name="warm")
        nc.vector.memset(warm[:], 0.0)
        warm2 = const.tile([P, 1], F32, name="warm2")
        nc.scalar.activation(out=warm2[:], in_=warm[:], func=ACTF.Exp)

        def copy_out(on_vector, dst, src):
            if on_vector:
                nc.vector.tensor_copy(out=dst, in_=src)
            else:
                nc.scalar.copy(out=dst, in_=src)

        def prep_k(b, hk, on_vector, pool=ps_p, tag="p"):
            if hk == 0:
                kt = prep.tile([P, HK, S], BF16, tag="kt")
                kt_t[b] = kt
            tp = pool.tile([P, S], BF16, tag=tag)

            def one(c):
                return lambda: nc.tensor.transpose(
                    out=tp[:, c * P : (c + 1) * P],
                    in_=kraw_t[b][:, c, hk * D : (hk + 1) * D],
                    identity=ident[:],
                )

            return [one(c) for c in range(8)], lambda: copy_out(on_vector, kt_t[b][:, hk, :], tp[:])

        def prep_q(b, on_vector, pool=ps_p, tag="p"):
            qt = prep.tile([P, 8, P], BF16, tag="qt")
            qt_t[b] = qt
            tp = pool.tile([P, S], BF16, tag=tag)

            def one(i):
                return lambda: nc.tensor.transpose(
                    out=tp[:, i * P : (i + 1) * P],
                    in_=qraw_t[b][:, i // 4, (i % 4) * D : (i % 4 + 1) * D],
                    identity=ident[:],
                )

            return [one(i) for i in range(8)], lambda: copy_out(
                on_vector, qt[:].rearrange("p i c -> p (i c)"), tp[:]
            )

        def prep_v(b):
            vg = prep.tile([P, 2, HK * D, 4], BF16, tag="vg", align_bytes=64)
            for g in range(2):
                nc.vector.tensor_copy(
                    out=vg[:, g, :, :].rearrange("p (c i) t -> p c t i", i=4),
                    in_=vraw_t[b][:, 4 * g : 4 * g + 4, :].rearrange("p t (c i) -> p c t i", i=4),
                )
            vcod = prep.tile([P, 2 * HK * D], U32, tag="vcod", align_bytes=64)
            vsc = prep.tile([P, 2 * HK * D], U8, tag="vsc", align_bytes=64)
            vcod_t[b], vsc_t[b] = vcod, vsc
            nc.vector.quantize_mx(
                out=vcod[:].bitcast(FP8X4),
                scales=vsc[:],
                in_=vg[:].rearrange("p g x t -> p (g x t)"),
            )

        st = {}
        gr = {}

        def unit(u):
            return u // 8, (u % 8) // 4, u % 4

        def permuted_copy(u):
            return u % 4 == 3 or u == NU - 2

        def stage_s_a(u):
            b, qb, h = unit(u)
            s_a = ps_s.tile([P, 512], F32, tag="s")
            nc.tensor.matmul(
                out=s_a[:],
                lhsT=qt_t[b][:, qb * 4 + h, :],
                rhs=kt_t[b][:, h // 2, 0:512],
                start=True,
                stop=True,
            )
            st[u] = {"s_a": s_a, "nb": 384 + qb * P}

        def stage_s_b(u):
            b, qb, h = unit(u)
            s_b = ps_s.tile([P, 512], F32, tag="s")
            nfree = st[u]["nb"] - P
            nc.tensor.matmul(
                out=s_b[:, 0:nfree],
                lhsT=qt_t[b][:, qb * 4 + h, :],
                rhs=kt_t[b][:, h // 2, 512 : 512 + nfree],
                start=True,
                stop=True,
            )
            st[u]["s_b"] = s_b

        def stage_s_d(u):
            b, qb, h = unit(u)
            s_b = st[u]["s_b"]
            nfree = st[u]["nb"] - P
            nc.tensor.matmul(
                out=s_b[:, nfree : nfree + P],
                lhsT=qt_t[b][:, qb * 4 + h, :],
                rhs=kt_t[b][:, h // 2, 512 + nfree : 512 + nfree + P],
                start=True,
                stop=False,
            )
            nc.tensor.matmul(
                out=s_b[:, nfree : nfree + P], lhsT=ident[:], rhs=mask[:], start=False, stop=True
            )

        def stage_m_a(u):
            d = st[u]
            ssb = work.tile([P, S], F32, tag="ssb")
            m0 = small.tile([P, 1], F32, tag="m0")
            nc.vector.tensor_scalar(
                out=ssb[:, 0:512],
                in0=d["s_a"][:],
                scalar1=-SCALING,
                scalar2=None,
                op0=ALU.mult,
                op1=ALU.min,
                accum_out=m0[:],
            )
            d["ssb"], d["m0"] = ssb, m0

        def stage_m_b(u):
            d = st[u]
            bias = small.tile([P, 1], F32, tag="bias")
            nc.vector.tensor_scalar(
                out=d["ssb"][:, 512 : 512 + d["nb"]],
                in0=d["s_b"][:, 0 : d["nb"]],
                scalar1=-SCALING,
                scalar2=d["m0"][:, 0:1],
                op0=ALU.mult,
                op1=ALU.min,
                accum_out=bias[:],
            )
            d["bias"] = bias

        def stage_e(u):
            b, qb, h = unit(u)
            d = st[u]
            if h == 0:
                ssum = small.tile([P, 4], F32, tag="ssum")
                gr[u // 4] = {"ssum": ssum}
            if qb == 0 and h == 3:
                e = ez
            else:
                e = work.tile([P, S], BF16, tag="e")
            n = 512 + d["nb"]
            nc.scalar.activation(
                out=e[:, 0:n],
                in_=d["ssb"][:, 0:n],
                func=ACTF.Exp,
                bias=d["bias"][:],
                scale=-1.0,
                accum_out=gr[u // 4]["ssum"][:, h : h + 1],
            )
            d["e"] = e

        def stage_t(u):
            b, qb, h = unit(u)
            d = st[u]
            tp = ps_t.tile([P, S], BF16, tag="t")
            d["tp"] = tp

            def one(j):
                return lambda: nc.tensor.transpose(
                    out=tp[:, j * P : (j + 1) * P],
                    in_=d["e"][:, j * P : (j + 1) * P],
                    identity=ident[:],
                )

            return [one(j) for j in range(8 if h == 3 else 4 + d["nb"] // P)]

        def stage_c(u):
            b, qb, h = unit(u)
            d = st[u]
            if permuted_copy(u):
                copy_out(
                    u == NU - 1,
                    gr[u // 4]["gq"][:, h, :, :, :],
                    d["tp"][:].rearrange("p (g t c) -> p g c t", g=2, t=4),
                )
            else:
                if qb == 0:
                    pl = plz[h]
                else:
                    pl = work.tile([P, S], BF16, tag="pl")
                n = 512 + d["nb"]
                nc.scalar.copy(out=pl[:, 0:n], in_=d["tp"][:, 0:n])
                d["pl"] = pl

        def stage_g(u):
            b, qb, h = unit(u)
            d = st[u]
            if h == 0:
                gq = one_buf.tile([P, 4, 2, P, 4], BF16, tag="gq", align_bytes=64)
                gr[u // 4]["gq"] = gq
            if not permuted_copy(u):
                nc.gpsimd.tensor_scalar(
                    out=gr[u // 4]["gq"][:, h, :, :, :],
                    in0=d["pl"][:].rearrange("p (g t c) -> p g c t", g=2, t=4),
                    scalar1=1.0,
                    scalar2=0.0,
                    op0=ALU.mult,
                    op1=ALU.add,
                )

        def stage_q(su, half):
            d = gr[su]
            if "ecod" not in d:
                ecod = two_buf.tile([P, 8 * P], U32, tag="ecod", align_bytes=64)
                esc = two_buf.tile([P, 8 * P], U8, tag="esc", align_bytes=64)
                d["ecod"], d["esc"] = ecod, esc
            cols = slice(half * 4 * P, (half + 1) * 4 * P)
            nc.vector.quantize_mx(
                out=d["ecod"][:, cols].bitcast(FP8X4),
                scales=d["esc"][:, cols],
                in_=d["gq"][:, 2 * half : 2 * half + 2, :, :, :].rearrange("p u g c t -> p (u g c t)"),
            )

        def stage_x(su):
            b = su // 2
            d = gr[su]
            o_ps = ps_o.tile([P, H * D], F32, tag="o")
            d["o_ps"] = o_ps
            for h in range(H):
                for g in range(2):
                    vcols = slice((g * HK + h // 2) * D, (g * HK + h // 2 + 1) * D)
                    ecols = slice((h * 2 + g) * P, (h * 2 + g + 1) * P)
                    nc.tensor.matmul_mx(
                        out=o_ps[:, h * D : (h + 1) * D],
                        lhsT=d["ecod"][:, ecols].bitcast(FP8X4),
                        lhsT_scale=d["esc"][:, ecols],
                        rhs=vcod_t[b][:, vcols].bitcast(FP8X4),
                        rhs_scale=vsc_t[b][:, vcols],
                        start=(g == 0),
                        stop=(g == 1),
                    )

        def stage_r(su):
            rinv = small.tile([P, 4], F32, tag="rinv")
            nc.vector.reciprocal(out=rinv[:], in_=gr[su]["ssum"][:])
            gr[su]["rinv"] = rinv

        def stage_n(su):
            b, qb = su // 2, su % 2
            o_sb = work.tile([P, H, D], F32, tag="o_sb")
            nc.vector.tensor_tensor(
                out=o_sb[:],
                in0=gr[su]["o_ps"][:].rearrange("p (h d) -> p h d", h=H),
                in1=gr[su]["rinv"][:].unsqueeze(2).to_broadcast([P, H, D]),
                op=ALU.mult,
            )
            r0 = b * E + qb * P
            nc.sync.dma_start(out=out[r0 : r0 + P, :], in_=o_sb[:].rearrange("p h d -> p (h d)"))

        def run(calls):
            for call in calls:
                call()

        def ok(u):
            return 0 <= u < NU

        first = prep_q(0, False, ps_t, "t")
        run(first[0])
        first[1]()
        first = prep_k(0, 0, True, ps_t, "t")
        run(first[0])
        first[1]()
        group = prep_k(0, 1, False)
        waiting = group[0]

        for step in range(-3, NU + 9):
            nxt = step // 8 + 1
            i = step % 8
            prepare = 0 <= step < NU and nxt < B
            if ok(step - 1):
                stage_e(step - 1)
            if ok(step + 2):
                stage_m_a(step + 2)
            if ok(step - 8) and (step - 8) % 4 == 0:
                stage_n((step - 8) // 4)
            if ok(step + 1):
                stage_m_b(step + 1)
            if step == 0:
                prep_v(0)
            tr = []
            if ok(step - 2):
                tr = stage_t(step - 2)
            if prepare and i in (0, 2, 4):
                if i == 0:
                    group = prep_k(nxt, 0, True)
                elif i == 2:
                    group = prep_q(nxt, nxt % 2 == 1)
                else:
                    group = prep_k(nxt, 1, False)
                waiting = group[0]
            late = 0 < len(waiting) <= 4
            tr = tr + waiting[0:4]
            waiting = waiting[4:]
            if ok(step + 3):
                stage_s_a(step + 3)
            run(tr[0:6])
            if ok(step + 2):
                stage_s_b(step + 2)
            run(tr[6:])
            if ok(step + 2):
                stage_s_d(step + 2)
            if ok(step - 7) and (step - 7) % 4 == 0:
                stage_x((step - 7) // 4)
            if ok(step - 3):
                stage_g(step - 3)
            if step == NU + 1:
                stage_q(NU // 4 - 1, 0)
            if ok(step - 2):
                stage_c(step - 2)
            if ok(step - 6) and (step - 6) % 4 == 0:
                su = (step - 6) // 4
                stage_q(su, 1)
                if prepare and i == 6:
                    prep_v(nxt)
                if su < NU // 4 - 1:
                    stage_q(su, 0)
                stage_r(su)
            if late:
                group[1]()
            if prepare and i == 0 and nxt + 2 < B:
                load(nxt + 2)
